import numpy as np
import ml_dtypes


def mxq(x, axis, fmt="e4m3"):
    dtype, down = {"e4m3": (ml_dtypes.float8_e4m3fn, 7), "e5m2": (ml_dtypes.float8_e5m2, 14)}[fmt]
    v = np.moveaxis(np.asarray(x, np.float32).astype(ml_dtypes.bfloat16).astype(np.float64), axis, -1)
    blocks = v.reshape(v.shape[:-1] + (-1, 32))
    amax = np.abs(blocks).max(-1, keepdims=True)
    byte = np.maximum(np.where(amax > 0, np.frexp(amax)[1] - 1 + 127, 0) - down, 1)
    scale = np.exp2(byte - 127.0)
    codes = (blocks / scale).astype(np.float32).astype(dtype).astype(np.float64)
    return np.moveaxis((codes * scale).reshape(v.shape), -1, axis)


WIDE = False


def mx_kscale(k):
    if not WIDE:
        return np.ones(k)
    levels = np.array([10, -10, 5, -5, 0])
    if k % 512:
        return np.exp2(np.random.permutation(np.resize(levels, k // 32))).repeat(32)
    a = np.empty((k // 512, 16))
    for p in range(k // 512):
        a[p, :8] = np.random.permutation(np.resize(levels, 8))
        for g in range(8):
            far = levels[np.abs(levels - a[p, g]) >= 10]
            a[p, g + 8] = far[np.random.randint(len(far))]
    return np.exp2(a.ravel()).repeat(32)


BF16 = ml_dtypes.bfloat16


def bf(x):
    return np.asarray(x, np.float32).astype(BF16)


def f64(x):
    return np.asarray(x).astype(np.float64)


L, B, P, H, DH, DM = 2, 8, 513, 8, 64, 512
M = L + 1
K = L * H * DH
R = P - 1
THR = 0.001


def sg(v):
    return v


def setup_inputs():
    s = mx_kscale(K).reshape(L, H, DH)
    return {
        "attn_cache": bf(np.random.standard_normal((L, B, P, H, DH)) * s[:, None, None]),
        "mlp_cache": bf(np.random.standard_normal((M, B, P, DM)) / np.sqrt(M)),
        "mlp_mask": bf(np.random.uniform(0.0, 1.0, (B, M))),
        "attn_mask": bf(np.random.uniform(0.0, 1.0, (B, L, H))),
        "modal_attention": bf(np.random.standard_normal((L, H, DH)) * s),
        "modal_mlp": bf(np.random.standard_normal((M, DM)) / np.sqrt(M)),
        "W_O": bf(np.random.standard_normal((L, H, DH, DM)) * 2.0 / np.sqrt(K) / s[..., None]),
        "post_bias": bf(np.random.standard_normal((L, DM)) * 0.3 / np.sqrt(L)),
        "orig_in": bf(np.random.standard_normal((B, P, DM))),
    }


def reference(attn_cache, mlp_cache, mlp_mask, attn_mask, modal_attention, modal_mlp, W_O, post_bias, orig_in):
    modal_attention = f64(modal_attention)
    modal_mlp = f64(modal_mlp)
    mm = f64(mlp_mask)[:, None, :, None]
    mlp_stack = np.moveaxis(f64(mlp_cache), 0, 2)
    out = (mm * mlp_stack).sum(axis=2)
    mlp_blend = np.where(mm < THR, (1.0 - mm) * modal_mlp, (1.0 - mm) * sg(modal_mlp))
    out = out + mlp_blend.sum(axis=2)
    am = f64(attn_mask)[:, None, :, :, None]
    attn_stack = np.moveaxis(f64(attn_cache), 0, 2)
    attn_blend = np.where(am < THR, (1.0 - am) * modal_attention, (1.0 - am) * sg(modal_attention))
    attn_term = am * attn_stack + attn_blend
    attn_term = attn_term[:, 1:].reshape(B, R, K)
    attn_term = mxq(attn_term, 2, "e4m3") @ mxq(f64(W_O).reshape(K, DM), 0, "e4m3")
    out = out[:, 1:] + attn_term + f64(post_bias).sum(axis=0)
    return np.concatenate([sg(f64(orig_in)[:, :1]), out], axis=1)

@@ -1,0 +1,281 @@
+from contextlib import ExitStack
+
+import concourse.mybir as mybir
+from concourse.masks import make_identity
+
+F32 = mybir.dt.float32
+BF16 = mybir.dt.bfloat16
+U32 = mybir.dt.uint32
+U8 = mybir.dt.uint8
+FP8X4 = mybir.dt.float8_e4m3fn_x4
+ALU = mybir.AluOpType
+ACT = mybir.ActivationFunctionType
+
+L, B, POS, H, DH, DM = 2, 8, 513, 8, 64, 512
+M = 3
+P = 128
+J = 4
+R = POS - 1
+KL = H * DH
+
+FLOPS = 2 * B * R * L * KL * DM
+BYTES = 2 * (L * B * R * KL + M * B * R * DM + L * KL * DM) + 4 * B * POS * DM
+
+PIN = False
+V_INTERLEAVE = ()
+
+
+def interleave(eng_copy, dst, src):
+    eng_copy(
+        out=dst.rearrange("p (c i) t -> p c t i", i=4),
+        in_=src.rearrange("p t (c i) -> p c t i", i=4),
+    )
+
+
+def tile_edgepruner_t_kernel(
+    tc, attn_cache, mlp_cache, mlp_mask, attn_mask, modal_attention, modal_mlp, W_O, post_bias, orig_in, out
+):
+    nc = tc.nc
+    with ExitStack() as ctx:
+        const = ctx.enter_context(tc.tile_pool(name="const", bufs=1))
+        apool = ctx.enter_context(tc.tile_pool(name="apool", bufs=4))
+        mpool = ctx.enter_context(tc.tile_pool(name="mpool", bufs=4))
+        opool = ctx.enter_context(tc.tile_pool(name="opool", bufs=3))
+        ppool = ctx.enter_context(tc.tile_pool(name="ppool", bufs=3))
+        gpool = ctx.enter_context(tc.tile_pool(name="gpool", bufs=3))
+        cpool = ctx.enter_context(tc.tile_pool(name="cpool", bufs=4))
+        psT = ctx.enter_context(tc.psum_pool(name="psT", bufs=4))
+        psO = ctx.enter_context(tc.psum_pool(name="psO", bufs=4))
+        if PIN:
+            ctx.enter_context(tc.manual_schedule())
+
+        xas = {}
+        xms = {}
+
+        def load_attn(b, fine):
+            xa = apool.tile([P, L, J, KL], BF16, name="xa")
+            xas[b] = xa
+            src = attn_cache[:, b, 1:POS, :, :].rearrange("l (p j) h d -> p l (j h d)", j=J)
+            dst = xa[:].rearrange("p l j k -> p l (j k)")
+            if fine:
+                return [(dst[:, l, :], src[:, l, :]) for l in range(L)]
+            return [(dst, src)]
+
+        def load_mlp(b, fine):
+            xm = mpool.tile([P, M, J, DM], BF16, name="xm")
+            xms[b] = xm
+            src = mlp_cache[:, b, 1:POS, :].rearrange("m (p j) n -> p m (j n)", j=J)
+            dst = xm[:].rearrange("p m j n -> p m (j n)")
+            if fine:
+                return [(dst[:, m, :], src[:, m, :]) for m in range(M)]
+            return [(dst, src)]
+
+        def issue(pairs):
+            for dst, src in pairs:
+                nc.sync.dma_start(out=dst, in_=src)
+
+        wraw = const.tile([P, L, 4, DM], BF16)
+        wsrc = W_O.rearrange("l h d n -> (l h d) n").rearrange("(l p t) n -> p l (t n)", l=L, p=P, t=4)
+        wdst = wraw[:].rearrange("p l t n -> p l (t n)")
+        a0 = load_attn(0, True)
+        m0 = load_mlp(0, True)
+        issue([(wdst[:, 0, :], wsrc[:, 0, :]), a0[0], (wdst[:, 1, :], wsrc[:, 1, :]), m0[0], a0[1], m0[1], m0[2]])
+
+        am_bc = const.tile([P, B * L * H], BF16)
+        nc.scalar.dma_start(out=am_bc[:], in_=attn_mask.rearrange("b l h -> (b l h)").partition_broadcast(P))
+        modalT = const.tile([P, L, 4], BF16)
+        with nc.allow_non_contiguous_dma(reason="256 eight-byte pieces, once"):
+            nc.scalar.dma_start(
+                out=modalT[:],
+                in_=modal_attention.rearrange("l h d -> (l h d)").rearrange("(l p t) -> p l t", l=L, p=P, t=4),
+            )
+        mmr = const.tile([B, M], BF16)
+        nc.scalar.dma_start(out=mmr[:], in_=mlp_mask)
+        mod8 = const.tile([B, M, DM], BF16)
+        nc.scalar.dma_start(
+            out=mod8[:].rearrange("b m n -> b (m n)"), in_=modal_mlp.rearrange("m n -> (m n)").partition_broadcast(B)
+        )
+        pb8 = const.tile([B, L, DM], BF16)
+        nc.scalar.dma_start(
+            out=pb8[:].rearrange("b l n -> b (l n)"), in_=post_bias.rearrange("l n -> (l n)").partition_broadcast(B)
+        )
+        mm_bc = const.tile([P, B * M], BF16)
+        nc.scalar.dma_start(out=mm_bc[:], in_=mlp_mask.rearrange("b m -> (b m)").partition_broadcast(P))
+        o8 = const.tile([B, DM], BF16)
+        nc.scalar.dma_start(out=o8[:], in_=orig_in[:, 0, :])
+
+        ident = const.tile([P, P], F32)
+        make_identity(nc, ident[:])
+
+        for b in range(1, min(4, 4)):
+            issue(load_attn(b, False))
+            issue(load_mlp(b, False))
+
+        crow = const.tile([P, DM], F32)
+        nc.vector.memset(crow[:], 0.0)
+        off = const.tile([P, H], F32)
+        nc.gpsimd.iota(off[:], pattern=[[-16, H]], base=0, channel_multiplier=1, allow_small_or_imprecise_dtypes=True)
+        low = const.tile([P, H], F32)
+        nc.vector.tensor_scalar(out=low[:], in0=off[:], scalar1=15.0, scalar2=None, op0=ALU.is_le)
+        head = const.tile([P, H], F32)
+        nc.vector.scalar_tensor_tensor(
+            out=head[:], in0=off[:], scalar=0.0, in1=low[:], op0=ALU.is_ge, op1=ALU.mult
+        )
+        sel = const.tile([P, B * L, H], F32)
+        nc.vector.tensor_tensor(
+            out=sel[:],
+            in0=am_bc[:].rearrange("p (c h) -> p c h", h=H),
+            in1=head[:].unsqueeze(1).to_broadcast([P, B * L, H]),
+            op=ALU.mult,
+        )
+        scl = const.tile([P, B, L], F32)
+        nc.vector.reduce_sum(scl[:].rearrange("p b l -> p (b l)"), sel[:], axis=mybir.AxisListType.X)
+        om = const.tile([P, B * L], F32)
+        nc.vector.tensor_scalar(
+            out=om[:], in0=scl[:].rearrange("p b l -> p (b l)"), scalar1=-1.0, scalar2=1.0, op0=ALU.mult, op1=ALU.add
+        )
+        bia = const.tile([P, B, L, 4], F32)
+        nc.vector.tensor_tensor(
+            out=bia[:],
+            in0=om[:].rearrange("p (b l) -> p b l", l=L).unsqueeze(3).to_broadcast([P, B, L, 4]),
+            in1=modalT[:].unsqueeze(1).to_broadcast([P, B, L, 4]),
+            op=ALU.mult,
+        )
+        omr = const.tile([B, M], F32)
+        nc.vector.tensor_scalar(out=omr[:], in0=mmr[:], scalar1=-1.0, scalar2=1.0, op0=ALU.mult, op1=ALU.add)
+        nc.vector.tensor_tensor(out=crow[0:B, :], in0=pb8[:, 0, :], in1=pb8[:, 1, :], op=ALU.add)
+        for m in range(M):
+            nc.vector.scalar_tensor_tensor(
+                out=crow[0:B, :], in0=mod8[:, m, :], scalar=omr[:, m : m + 1], in1=crow[0:B, :], op0=ALU.mult, op1=ALU.add
+            )
+        mmf = const.tile([P, B * M], F32)
+        nc.vector.tensor_copy(out=mmf[:], in_=mm_bc[:])
+
+        cbc = const.tile([P, B, DM], F32)
+
+        def spread_const(b):
+            po = psO.tile([P, DM], F32, name="po")
+            nc.tensor.matmul(out=po[:], lhsT=ident[:, b : b + 1].to_broadcast([P, P]), rhs=crow[:], start=True, stop=True)
+            nc.scalar.copy(out=cbc[:, b, :], in_=po[:])
+
+        wg = const.tile([P, L, DM, 4], BF16, align_bytes=64)
+        wc = const.tile([P, L, DM], U32, align_bytes=64)
+        ws = const.tile([P, L, DM], U8, align_bytes=64)
+
+        def w_regroup(l, eng_copy):
+            interleave(eng_copy, wg[:, l], wraw[:, l])
+
+        def w_quant(l):
+            nc.vector.quantize_mx(
+                out=wc[:, l, :].bitcast(FP8X4), scales=ws[:, l, :], in_=wg[:, l].rearrange("p n t -> p (n t)")
+            )
+
+        codes = {}
+        accs = {}
+
+        def t1(b, l):
+            xa = xas[b]
+            planes = ppool.tile([P, 4, J * P], BF16, name="planes")
+            for u in range(2):
+                pt = psT.tile([P, J, P], F32, name="pt")
+                for j in range(J):
+                    nc.tensor.transpose(
+                        out=pt[:, j, :], in_=xa[:, l, j, :].bitcast(F32)[:, u : 2 * P : 2], identity=ident[:]
+                    )
+                ptv = pt[:].rearrange("p j r -> p (j r)").bitcast(BF16).rearrange("p (c e) -> p c e", e=2)
+                for e in range(2):
+                    nc.scalar.activation(
+                        out=planes[:, 2 * u + e, :],
+                        in_=ptv[:, :, e],
+                        func=ACT.Identity,
+                        bias=bia[:, b, l, 2 * u + e : 2 * u + e + 1],
+                        scale=scl[:, b, l : l + 1],
+                    )
+            grp = gpool.tile([P, J * P, 4], BF16, align_bytes=64, name="grp")
+            if (b, l) in V_INTERLEAVE:
+                interleave(nc.vector.tensor_copy, grp[:], planes[:])
+            else:
+                interleave(nc.scalar.copy, grp[:], planes[:])
+            return grp
+
+        def quant(b, l, grp):
+            ac = cpool.tile([P, J * P], U32, align_bytes=64, name="ac")
+            asc = cpool.tile([P, J * P], U8, align_bytes=64, name="asc")
+            nc.vector.quantize_mx(out=ac[:].bitcast(FP8X4), scales=asc[:], in_=grp[:].rearrange("p c t -> p (c t)"))
+            codes[(b, l)] = (ac, asc)
+
+        def stt(b, m):
+            if m == 0:
+                acc = opool.tile([P, J, DM], F32, name="acc")
+                accs[b] = acc
+                other = cbc[:, b, :].unsqueeze(1).to_broadcast([P, J, DM])
+            else:
+                acc = accs[b]
+                other = acc[:]
+            nc.vector.scalar_tensor_tensor(
+                out=acc[:],
+                in0=xms[b][:, m],
+                scalar=mmf[:, M * b + m : M * b + m + 1],
+                in1=other,
+                op0=ALU.mult,
+                op1=ALU.add,
+            )
+
+        def mx(b, fine_store):
+            acc = accs[b]
+            dst = out[b, 1:POS, :].rearrange("(p j) n -> p j n", j=J)
+            pos = []
+            for j in range(J):
+                po = psO.tile([P, DM], F32, name="po")
+                pos.append(po)
+                for l in range(L):
+                    ac, asc = codes[(b, l)]
+                    nc.tensor.matmul_mx(
+                        out=po[:],
+                        lhsT=ac[:, P * j : P * j + P].bitcast(FP8X4),
+                        lhsT_scale=asc[:, P * j : P * j + P],
+                        rhs=wc[:, l, :].bitcast(FP8X4),
+                        rhs_scale=ws[:, l, :],
+                        start=(l == 0),
+                        stop=(l == L - 1),
+                    )
+            for j in range(J):
+                nc.vector.tensor_tensor(out=acc[:, j, :], in0=acc[:, j, :], in1=pos[j][:], op=ALU.add)
+                if fine_store and j % 2 == 1:
+                    nc.sync.dma_start(out=dst[:, j - 1 : j + 1, :], in_=acc[:, j - 1 : j + 1, :])
+            if not fine_store:
+                nc.sync.dma_start(out=dst, in_=acc[:])
+
+        w_regroup(0, nc.vector.tensor_copy)
+        g00 = t1(0, 0)
+        w_regroup(1, nc.scalar.copy)
+        for b in range(B):
+            spread_const(b)
+        w_quant(0)
+        w_quant(1)
+        quant(0, 0, g00)
+        stt(0, 0)
+        g01 = t1(0, 1)
+        quant(0, 1, g01)
+        o8f = const.tile([B, DM], F32)
+        nc.vector.tensor_copy(out=o8f[:], in_=o8[:])
+        nc.scalar.dma_start(out=out[:, 0, :], in_=o8f[:])
+
+        ahead = min(4, 4)
+        for b in range(B):
+            nxt = b + 1
+            if nxt < B:
+                ga = t1(nxt, 0)
+            if b > 0:
+                stt(b, 0)
+            if nxt < B:
+                quant(nxt, 0, ga)
+                gb = t1(nxt, 1)
+            stt(b, 1)
+            stt(b, 2)
+            if nxt < B:
+                quant(nxt, 1, gb)
+            if b + ahead < B:
+                issue(load_attn(b + ahead, False))
+                issue(load_mlp(b + ahead, False))
+            mx(b, b == B - 1)

@@ -15,14 +15,14 @@ L, B, POS, H, DH, DM = 2, 8, 513, 8, 64, 512
 M = 3
 P = 128
 J = 4
+NB = DM // P
 R = POS - 1
+AHEAD = 5
+LAG = 0
 KL = H * DH
 
 FLOPS = 2 * B * R * L * KL * DM
 BYTES = 2 * (L * B * R * KL + M * B * R * DM + L * KL * DM) + 4 * B * POS * DM
-
-PIN = False
-V_INTERLEAVE = ()
 
 
 def interleave(eng_copy, dst, src):
@@ -32,22 +32,30 @@ def interleave(eng_copy, dst, src):
     )
 
 
+def interleave_on_vector(h):
+    return h < 2 or h % 8 in (0, 2, 3, 5, 6)
+
+
+def product_on_tensor(b, j):
+    return j < 3 or b == B - 1
+
+
 def tile_edgepruner_t_kernel(
     tc, attn_cache, mlp_cache, mlp_mask, attn_mask, modal_attention, modal_mlp, W_O, post_bias, orig_in, out
 ):
     nc = tc.nc
     with ExitStack() as ctx:
         const = ctx.enter_context(tc.tile_pool(name="const", bufs=1))
-        apool = ctx.enter_context(tc.tile_pool(name="apool", bufs=4))
-        mpool = ctx.enter_context(tc.tile_pool(name="mpool", bufs=4))
-        opool = ctx.enter_context(tc.tile_pool(name="opool", bufs=3))
+        apool = ctx.enter_context(tc.tile_pool(name="apool", bufs=5))
+        mpool = ctx.enter_context(tc.tile_pool(name="mpool", bufs=7))
+        opool = ctx.enter_context(tc.tile_pool(name="opool", bufs=5))
+        zpool = ctx.enter_context(tc.tile_pool(name="zpool", bufs=2))
         ppool = ctx.enter_context(tc.tile_pool(name="ppool", bufs=3))
-        gpool = ctx.enter_context(tc.tile_pool(name="gpool", bufs=3))
-        cpool = ctx.enter_context(tc.tile_pool(name="cpool", bufs=4))
-        psT = ctx.enter_context(tc.psum_pool(name="psT", bufs=4))
-        psO = ctx.enter_context(tc.psum_pool(name="psO", bufs=4))
-        if PIN:
-            ctx.enter_context(tc.manual_schedule())
+        gpool = ctx.enter_context(tc.tile_pool(name="gpool", bufs=4))
+        cpool = ctx.enter_context(tc.tile_pool(name="cpool", bufs=5))
+        psT = ctx.enter_context(tc.psum_pool(name="psT", bufs=3))
+        psZ = ctx.enter_context(tc.psum_pool(name="psZ", bufs=2))
+        psO = ctx.enter_context(tc.psum_pool(name="psO", bufs=3))
 
         xas = {}
         xms = {}
@@ -74,208 +82,268 @@ def tile_edgepruner_t_kernel(
             for dst, src in pairs:
                 nc.sync.dma_start(out=dst, in_=src)
 
-        wraw = const.tile([P, L, 4, DM], BF16)
-        wsrc = W_O.rearrange("l h d n -> (l h d) n").rearrange("(l p t) n -> p l (t n)", l=L, p=P, t=4)
-        wdst = wraw[:].rearrange("p l t n -> p l (t n)")
-        a0 = load_attn(0, True)
-        m0 = load_mlp(0, True)
-        issue([(wdst[:, 0, :], wsrc[:, 0, :]), a0[0], (wdst[:, 1, :], wsrc[:, 1, :]), m0[0], a0[1], m0[1], m0[2]])
-
-        am_bc = const.tile([P, B * L * H], BF16)
-        nc.scalar.dma_start(out=am_bc[:], in_=attn_mask.rearrange("b l h -> (b l h)").partition_broadcast(P))
-        modalT = const.tile([P, L, 4], BF16)
-        with nc.allow_non_contiguous_dma(reason="256 eight-byte pieces, once"):
+        with tc.manual_schedule():
+            am_bc = const.tile([P, B * L * H], BF16)
+            nc.sync.dma_start(out=am_bc[:], in_=attn_mask.rearrange("b l h -> (b l h)").partition_broadcast(P))
+            modalT = const.tile([P, L, 4], BF16)
+            with nc.allow_non_contiguous_dma(reason="256 eight-byte pieces, once"):
+                nc.sync.dma_start(
+                    out=modalT[:],
+                    in_=modal_attention.rearrange("l h d -> (l h d)").rearrange("(l p t) -> p l t", l=L, p=P, t=4),
+                )
+            wraw = mpool.tile([P, L, 4, DM], BF16, name="xm")
+            wsrc = W_O.rearrange("l h d n -> (l h d) n").rearrange("(l p t) n -> p l (t n)", l=L, p=P, t=4)
+            wdst = wraw[:].rearrange("p l t n -> p l (t n)")
+            a0 = load_attn(0, True)
+            m0 = load_mlp(0, True)
+            issue([a0[0], (wdst[:, 0, :], wsrc[:, 0, :]), a0[1], (wdst[:, 1, :], wsrc[:, 1, :])])
+            mm_bc = const.tile([P, B, M], BF16)
             nc.scalar.dma_start(
-                out=modalT[:],
-                in_=modal_attention.rearrange("l h d -> (l h d)").rearrange("(l p t) -> p l t", l=L, p=P, t=4),
+                out=mm_bc[:].rearrange("p b m -> p (b m)"), in_=mlp_mask.rearrange("b m -> (b m)").partition_broadcast(P)
             )
-        mmr = const.tile([B, M], BF16)
-        nc.scalar.dma_start(out=mmr[:], in_=mlp_mask)
-        mod8 = const.tile([B, M, DM], BF16)
-        nc.scalar.dma_start(
-            out=mod8[:].rearrange("b m n -> b (m n)"), in_=modal_mlp.rearrange("m n -> (m n)").partition_broadcast(B)
-        )
-        pb8 = const.tile([B, L, DM], BF16)
-        nc.scalar.dma_start(
-            out=pb8[:].rearrange("b l n -> b (l n)"), in_=post_bias.rearrange("l n -> (l n)").partition_broadcast(B)
-        )
-        mm_bc = const.tile([P, B * M], BF16)
-        nc.scalar.dma_start(out=mm_bc[:], in_=mlp_mask.rearrange("b m -> (b m)").partition_broadcast(P))
-        o8 = const.tile([B, DM], BF16)
-        nc.scalar.dma_start(out=o8[:], in_=orig_in[:, 0, :])
+            rows = const.tile([P, DM], BF16)
+            nc.gpsimd.memset(rows[:], 0.0)
+            nc.scalar.dma_start(out=rows[0:M, :], in_=modal_mlp)
+            nc.scalar.dma_start(out=rows[M : M + L, :], in_=post_bias)
+            a1 = load_attn(1, True)
+            issue(a1)
+            issue([m0[1], m0[0], m0[2]])
+            o8 = const.tile([B, DM], BF16)
+            nc.sync.dma_start(out=o8[:], in_=orig_in[:, 0, :])
+            for b in range(2, AHEAD):
+                issue(load_attn(b, False))
+                issue(load_mlp(b - 1, False))
 
-        ident = const.tile([P, P], F32)
-        make_identity(nc, ident[:])
+            ident = const.tile([P, P], F32)
+            make_identity(nc, ident[:])
+            off = const.tile([P, H], F32)
+            nc.gpsimd.iota(off[:], pattern=[[-16, H]], base=0, channel_multiplier=1, allow_small_or_imprecise_dtypes=True)
+            warm = const.tile([P, 1], F32)
+            nc.scalar.activation(out=warm[:], in_=ident[:, 0:1], func=ACT.Identity, scale=1.0)
+            identb = const.tile([P, P], BF16)
+            make_identity(nc, identb[:])
 
-        for b in range(1, min(4, 4)):
-            issue(load_attn(b, False))
-            issue(load_mlp(b, False))
-
-        crow = const.tile([P, DM], F32)
-        nc.vector.memset(crow[:], 0.0)
-        off = const.tile([P, H], F32)
-        nc.gpsimd.iota(off[:], pattern=[[-16, H]], base=0, channel_multiplier=1, allow_small_or_imprecise_dtypes=True)
-        low = const.tile([P, H], F32)
-        nc.vector.tensor_scalar(out=low[:], in0=off[:], scalar1=15.0, scalar2=None, op0=ALU.is_le)
-        head = const.tile([P, H], F32)
-        nc.vector.scalar_tensor_tensor(
-            out=head[:], in0=off[:], scalar=0.0, in1=low[:], op0=ALU.is_ge, op1=ALU.mult
-        )
-        sel = const.tile([P, B * L, H], F32)
-        nc.vector.tensor_tensor(
-            out=sel[:],
-            in0=am_bc[:].rearrange("p (c h) -> p c h", h=H),
-            in1=head[:].unsqueeze(1).to_broadcast([P, B * L, H]),
-            op=ALU.mult,
-        )
-        scl = const.tile([P, B, L], F32)
-        nc.vector.reduce_sum(scl[:].rearrange("p b l -> p (b l)"), sel[:], axis=mybir.AxisListType.X)
-        om = const.tile([P, B * L], F32)
-        nc.vector.tensor_scalar(
-            out=om[:], in0=scl[:].rearrange("p b l -> p (b l)"), scalar1=-1.0, scalar2=1.0, op0=ALU.mult, op1=ALU.add
-        )
-        bia = const.tile([P, B, L, 4], F32)
-        nc.vector.tensor_tensor(
-            out=bia[:],
-            in0=om[:].rearrange("p (b l) -> p b l", l=L).unsqueeze(3).to_broadcast([P, B, L, 4]),
-            in1=modalT[:].unsqueeze(1).to_broadcast([P, B, L, 4]),
-            op=ALU.mult,
-        )
-        omr = const.tile([B, M], F32)
-        nc.vector.tensor_scalar(out=omr[:], in0=mmr[:], scalar1=-1.0, scalar2=1.0, op0=ALU.mult, op1=ALU.add)
-        nc.vector.tensor_tensor(out=crow[0:B, :], in0=pb8[:, 0, :], in1=pb8[:, 1, :], op=ALU.add)
-        for m in range(M):
-            nc.vector.scalar_tensor_tensor(
-                out=crow[0:B, :], in0=mod8[:, m, :], scalar=omr[:, m : m + 1], in1=crow[0:B, :], op0=ALU.mult, op1=ALU.add
+            low = const.tile([P, H], F32)
+            nc.vector.tensor_scalar(out=low[:], in0=off[:], scalar1=15.0, scalar2=None, op0=ALU.is_le)
+            head = const.tile([P, H], F32)
+            nc.vector.scalar_tensor_tensor(out=head[:], in0=off[:], scalar=0.0, in1=low[:], op0=ALU.is_ge, op1=ALU.mult)
+            sel = const.tile([P, B * L, H], F32)
+            nc.vector.tensor_tensor(
+                out=sel[:],
+                in0=am_bc[:].rearrange("p (c h) -> p c h", h=H),
+                in1=head[:].unsqueeze(1).to_broadcast([P, B * L, H]),
+                op=ALU.mult,
             )
-        mmf = const.tile([P, B * M], F32)
-        nc.vector.tensor_copy(out=mmf[:], in_=mm_bc[:])
-
-        cbc = const.tile([P, B, DM], F32)
-
-        def spread_const(b):
-            po = psO.tile([P, DM], F32, name="po")
-            nc.tensor.matmul(out=po[:], lhsT=ident[:, b : b + 1].to_broadcast([P, P]), rhs=crow[:], start=True, stop=True)
-            nc.scalar.copy(out=cbc[:, b, :], in_=po[:])
-
-        wg = const.tile([P, L, DM, 4], BF16, align_bytes=64)
-        wc = const.tile([P, L, DM], U32, align_bytes=64)
-        ws = const.tile([P, L, DM], U8, align_bytes=64)
-
-        def w_regroup(l, eng_copy):
-            interleave(eng_copy, wg[:, l], wraw[:, l])
-
-        def w_quant(l):
-            nc.vector.quantize_mx(
-                out=wc[:, l, :].bitcast(FP8X4), scales=ws[:, l, :], in_=wg[:, l].rearrange("p n t -> p (n t)")
+            scl = const.tile([P, B, L], F32)
+            nc.vector.reduce_sum(scl[:].rearrange("p b l -> p (b l)"), sel[:], axis=mybir.AxisListType.X)
+            om = const.tile([P, B * L], F32)
+            nc.vector.tensor_scalar(
+                out=om[:], in0=scl[:].rearrange("p b l -> p (b l)"), scalar1=-1.0, scalar2=1.0, op0=ALU.mult, op1=ALU.add
+            )
+            bia = const.tile([P, B, L, 4], F32)
+            nc.vector.tensor_tensor(
+                out=bia[:],
+                in0=om[:].rearrange("p (b l) -> p b l", l=L).unsqueeze(3).to_broadcast([P, B, L, 4]),
+                in1=modalT[:].unsqueeze(1).to_broadcast([P, B, L, 4]),
+                op=ALU.mult,
             )
 
-        codes = {}
-        accs = {}
+            diag = const.tile([P, B, P], BF16)
+            nc.gpsimd.tensor_tensor(
+                out=diag[:],
+                in0=identb[:].unsqueeze(1).to_broadcast([P, B, P]),
+                in1=mm_bc[:, :, 0:1].to_broadcast([P, B, P]),
+                op=ALU.mult,
+            )
+            mmf = const.tile([P, B * M], F32)
+            cT = const.tile([P, NB, B], F32)
 
-        def t1(b, l):
-            xa = xas[b]
-            planes = ppool.tile([P, 4, J * P], BF16, name="planes")
-            for u in range(2):
-                pt = psT.tile([P, J, P], F32, name="pt")
-                for j in range(J):
-                    nc.tensor.transpose(
-                        out=pt[:, j, :], in_=xa[:, l, j, :].bitcast(F32)[:, u : 2 * P : 2], identity=ident[:]
+            def const_columns():
+                pc = psO.tile([P, NB, P], BF16, name="po")
+                for nb in range(NB):
+                    nc.tensor.transpose(out=pc[:, nb, :], in_=rows[:, P * nb : P * nb + P], identity=identb[:])
+                rT = const.tile([P, NB, M + L], F32)
+                nc.vector.tensor_copy(out=rT[:], in_=pc[:, :, 0 : M + L])
+                omm = const.tile([P, B, M], F32)
+                nc.vector.tensor_scalar(out=omm[:], in0=mm_bc[:], scalar1=-1.0, scalar2=1.0, op0=ALU.mult, op1=ALU.add)
+                pbT = const.tile([P, NB], F32)
+                nc.vector.reduce_sum(pbT[:], rT[:, :, M : M + L], axis=mybir.AxisListType.X)
+                nc.vector.tensor_copy(out=mmf[:], in_=mm_bc[:].rearrange("p b m -> p (b m)"))
+                ct3 = const.tile([P, NB, B, M], F32)
+                for nb in range(NB):
+                    nc.vector.tensor_tensor(
+                        out=ct3[:, nb], in0=omm[:], in1=rT[:, nb : nb + 1, 0:M].to_broadcast([P, B, M]), op=ALU.mult
                     )
-                ptv = pt[:].rearrange("p j r -> p (j r)").bitcast(BF16).rearrange("p (c e) -> p c e", e=2)
-                for e in range(2):
-                    nc.scalar.activation(
-                        out=planes[:, 2 * u + e, :],
-                        in_=ptv[:, :, e],
-                        func=ACT.Identity,
-                        bias=bia[:, b, l, 2 * u + e : 2 * u + e + 1],
-                        scale=scl[:, b, l : l + 1],
-                    )
-            grp = gpool.tile([P, J * P, 4], BF16, align_bytes=64, name="grp")
-            if (b, l) in V_INTERLEAVE:
-                interleave(nc.vector.tensor_copy, grp[:], planes[:])
-            else:
-                interleave(nc.scalar.copy, grp[:], planes[:])
-            return grp
+                ct1 = const.tile([P, NB, B], F32)
+                nc.vector.reduce_sum(ct1[:], ct3[:], axis=mybir.AxisListType.X)
+                nc.vector.tensor_tensor(
+                    out=cT[:], in0=ct1[:], in1=pbT[:].unsqueeze(2).to_broadcast([P, NB, B]), op=ALU.add
+                )
 
-        def quant(b, l, grp):
-            ac = cpool.tile([P, J * P], U32, align_bytes=64, name="ac")
-            asc = cpool.tile([P, J * P], U8, align_bytes=64, name="asc")
-            nc.vector.quantize_mx(out=ac[:].bitcast(FP8X4), scales=asc[:], in_=grp[:].rearrange("p c t -> p (c t)"))
-            codes[(b, l)] = (ac, asc)
+            wc = const.tile([P, L, DM], U32, align_bytes=64)
+            ws = const.tile([P, L, DM], U8, align_bytes=64)
 
-        def stt(b, m):
-            if m == 0:
-                acc = opool.tile([P, J, DM], F32, name="acc")
-                accs[b] = acc
-                other = cbc[:, b, :].unsqueeze(1).to_broadcast([P, J, DM])
-            else:
-                acc = accs[b]
-                other = acc[:]
-            nc.vector.scalar_tensor_tensor(
-                out=acc[:],
-                in0=xms[b][:, m],
-                scalar=mmf[:, M * b + m : M * b + m + 1],
-                in1=other,
-                op0=ALU.mult,
-                op1=ALU.add,
-            )
+            wgs = {}
 
-        def mx(b, fine_store):
-            acc = accs[b]
-            dst = out[b, 1:POS, :].rearrange("(p j) n -> p j n", j=J)
-            pos = []
-            for j in range(J):
-                po = psO.tile([P, DM], F32, name="po")
-                pos.append(po)
+            def w_regroup(l):
+                grp = gpool.tile([P, DM, 4], BF16, align_bytes=64, name="grp")
+                wgs[l] = grp
+                interleave(nc.vector.tensor_copy, grp[:], wraw[:, l])
+
+            def w_quant(l):
+                nc.vector.quantize_mx(
+                    out=wc[:, l, :].bitcast(FP8X4), scales=ws[:, l, :], in_=wgs[l][:].rearrange("p n t -> p (n t)")
+                )
+
+            banks = {}
+            planes = {}
+            grps = {}
+            codes = {}
+            zs = {}
+            pos = {}
+            accs = {}
+
+            def turn(h):
+                b, l = divmod(h, L)
+                for u in range(2):
+                    pt = psT.tile([P, J, P], F32, name="pt")
+                    banks[h, u] = pt
+                    for j in range(J):
+                        nc.tensor.transpose(
+                            out=pt[:, j, :], in_=xas[b][:, l, j, :].bitcast(F32)[:, u : 2 * P : 2], identity=ident[:]
+                        )
+
+            def blend(h):
+                b, l = divmod(h, L)
+                pl = ppool.tile([P, 4, J * P], BF16, name="pl")
+                planes[h] = pl
+                for u in range(2):
+                    ptv = banks[h, u][:].rearrange("p j r -> p (j r)").bitcast(BF16).rearrange("p (c e) -> p c e", e=2)
+                    for e in range(2):
+                        nc.scalar.activation(
+                            out=pl[:, 2 * u + e, :],
+                            in_=ptv[:, :, e],
+                            func=ACT.Identity,
+                            bias=bia[:, b, l, 2 * u + e : 2 * u + e + 1],
+                            scale=scl[:, b, l : l + 1],
+                        )
+
+            def regroup(h, eng_copy):
+                grp = gpool.tile([P, J * P, 4], BF16, align_bytes=64, name="grp")
+                grps[h] = grp
+                interleave(eng_copy, grp[:], planes[h][:])
+
+            def quant(h):
+                ac = cpool.tile([P, J * P], U32, align_bytes=64, name="ac")
+                asc = cpool.tile([P, J * P], U8, align_bytes=64, name="asc")
+                nc.vector.quantize_mx(out=ac[:].bitcast(FP8X4), scales=asc[:], in_=grps[h][:].rearrange("p c t -> p (c t)"))
+                codes[h] = (ac, asc)
+
+            def mx(b, nb):
+                if nb == 0:
+                    z = zpool.tile([P, NB, J * P], F32, name="z")
+                    zs[b] = z
+                pz = psZ.tile([P, J * P], F32, name="pz")
                 for l in range(L):
-                    ac, asc = codes[(b, l)]
+                    ac, asc = codes[L * b + l]
                     nc.tensor.matmul_mx(
-                        out=po[:],
-                        lhsT=ac[:, P * j : P * j + P].bitcast(FP8X4),
-                        lhsT_scale=asc[:, P * j : P * j + P],
-                        rhs=wc[:, l, :].bitcast(FP8X4),
-                        rhs_scale=ws[:, l, :],
+                        out=pz[:],
+                        lhsT=wc[:, l, P * nb : P * nb + P].bitcast(FP8X4),
+                        lhsT_scale=ws[:, l, P * nb : P * nb + P],
+                        rhs=ac[:].bitcast(FP8X4),
+                        rhs_scale=asc[:],
                         start=(l == 0),
                         stop=(l == L - 1),
                     )
-            for j in range(J):
-                nc.vector.tensor_tensor(out=acc[:, j, :], in0=acc[:, j, :], in1=pos[j][:], op=ALU.add)
-                if fine_store and j % 2 == 1:
-                    nc.sync.dma_start(out=dst[:, j - 1 : j + 1, :], in_=acc[:, j - 1 : j + 1, :])
-            if not fine_store:
-                nc.sync.dma_start(out=dst, in_=acc[:])
+                nc.scalar.activation(out=zs[b][:, nb, :], in_=pz[:], func=ACT.Identity, bias=cT[:, nb, b : b + 1], scale=1.0)
 
-        w_regroup(0, nc.vector.tensor_copy)
-        g00 = t1(0, 0)
-        w_regroup(1, nc.scalar.copy)
-        for b in range(B):
-            spread_const(b)
-        w_quant(0)
-        w_quant(1)
-        quant(0, 0, g00)
-        stt(0, 0)
-        g01 = t1(0, 1)
-        quant(0, 1, g01)
-        o8f = const.tile([B, DM], F32)
-        nc.vector.tensor_copy(out=o8f[:], in_=o8[:])
-        nc.scalar.dma_start(out=out[:, 0, :], in_=o8f[:])
+            def back(b, j):
+                on_pe = product_on_tensor(b, j)
+                po = psO.tile([P, NB, P], F32, name="po")
+                pos[b, j] = po
+                if on_pe:
+                    nc.tensor.matmul(
+                        out=po[:].rearrange("p a n -> p (a n)"), lhsT=diag[:, b, :], rhs=xms[b][:, 0, j, :], start=True, stop=False
+                    )
+                for nb in range(NB):
+                    nc.tensor.matmul(
+                        out=po[:, nb, :],
+                        lhsT=zs[b][:, nb, P * j : P * j + P],
+                        rhs=ident[:],
+                        start=not on_pe,
+                        stop=(not on_pe or nb == NB - 1),
+                        is_transpose=True,
+                    )
 
-        ahead = min(4, 4)
-        for b in range(B):
-            nxt = b + 1
-            if nxt < B:
-                ga = t1(nxt, 0)
-            if b > 0:
-                stt(b, 0)
-            if nxt < B:
-                quant(nxt, 0, ga)
-                gb = t1(nxt, 1)
-            stt(b, 1)
-            stt(b, 2)
-            if nxt < B:
-                quant(nxt, 1, gb)
-            if b + ahead < B:
-                issue(load_attn(b + ahead, False))
-                issue(load_mlp(b + ahead, False))
-            mx(b, b == B - 1)
+            def term(b, m, acc, js, other):
+                nc.vector.scalar_tensor_tensor(
+                    out=acc,
+                    in0=xms[b][:, m, js, :],
+                    scalar=mmf[:, M * b + m : M * b + m + 1],
+                    in1=other,
+                    op0=ALU.mult,
+                    op1=ALU.add,
+                )
+
+            def first_terms(b, j):
+                half, jj = divmod(j, 2)
+                if jj == 0:
+                    acc = opool.tile([P, 2, DM], F32, name="acc")
+                    accs[b, half] = acc
+                acc = accs[b, half][:, jj : jj + 1, :]
+                js = slice(j, j + 1)
+                term(b, 1, acc, js, pos[b, j][:].rearrange("p a n -> p (a n)").unsqueeze(1))
+                if not product_on_tensor(b, j):
+                    term(b, 0, acc, js, acc)
+
+            def last_term(b, half):
+                acc = accs[b, half]
+                js = slice(2 * half, 2 * half + 2)
+                term(b, 2, acc[:], js, acc[:])
+                dst = out[b, 1:POS, :].rearrange("(p j) n -> p j n", j=J)
+                nc.sync.dma_start(out=dst[:, js, :], in_=acc[:])
+
+            turn(0)
+            blend(0)
+            w_regroup(0)
+            const_columns()
+            w_quant(0)
+            o8f = const.tile([B, DM], F32)
+            nc.gpsimd.tensor_copy(out=o8f[:], in_=o8[:])
+
+        for h in range(L * B + 5 + LAG):
+            hv = h - LAG
+            bx, half = divmod(hv - 2, 2)
+            bd = bx - 1
+            if h + 1 < L * B:
+                turn(h + 1)
+                blend(h + 1)
+            if 0 <= bx < B:
+                for nb in (2 * half, 2 * half + 1):
+                    mx(bx, nb)
+            if 0 <= bd < B:
+                for j in (2 * half, 2 * half + 1):
+                    back(bd, j)
+            if h + 1 < L * B and not interleave_on_vector(h + 1):
+                regroup(h + 1, nc.scalar.copy)
+            if 0 <= hv < L * B and interleave_on_vector(hv):
+                regroup(hv, nc.vector.tensor_copy)
+            if hv == 0:
+                w_regroup(1)
+            if hv - 5 >= 0:
+                last_term(*divmod(hv - 5, 2))
+            if 0 <= hv < L * B:
+                quant(hv)
+            if hv == 0:
+                w_quant(1)
+            if 0 <= bd < B:
+                for j in (2 * half, 2 * half + 1):
+                    first_terms(bd, j)
+            if h % 2 == 1:
+                b = h // 2
+                if b + AHEAD < B:
+                    issue(load_attn(b + AHEAD, False))
+                if b + AHEAD - 1 < B:
+                    issue(load_mlp(b + AHEAD - 1, False))
+            if h == 4:
+                nc.sync.dma_start(out=out[:, 0, :], in_=o8f[:])

@@ -13,6 +13,8 @@ ACT = mybir.ActivationFunctionType
 
 L, B, POS, H, DH, DM = 2, 8, 513, 8, 64, 512
 M = 3
+NAM = B * L * H
+R_ATT, R_MLP, R_PB = 0, L, L + M
 P = 128
 J = 4
 NB = DM // P
@@ -33,11 +35,11 @@ def interleave(eng_copy, dst, src):
 
 
 def interleave_on_vector(h):
-    return h < 2 or h % 8 in (0, 2, 3, 5, 6)
+    return h < 2 or h % 8 in (0, 1, 3, 4, 5, 7)
 
 
 def product_on_tensor(b, j):
-    return j < 3 or b == B - 1
+    return b > 0 and (j < 3 or b >= 4)
 
 
 def tile_edgepruner_t_kernel(
@@ -56,6 +58,7 @@ def tile_edgepruner_t_kernel(
         psT = ctx.enter_context(tc.psum_pool(name="psT", bufs=3))
         psZ = ctx.enter_context(tc.psum_pool(name="psZ", bufs=2))
         psO = ctx.enter_context(tc.psum_pool(name="psO", bufs=3))
+        ctx.enter_context(tc.manual_schedule())
 
         xas = {}
         xms = {}
@@ -82,234 +85,248 @@ def tile_edgepruner_t_kernel(
             for dst, src in pairs:
                 nc.sync.dma_start(out=dst, in_=src)
 
-        with tc.manual_schedule():
-            am_bc = const.tile([P, B * L * H], BF16)
-            nc.sync.dma_start(out=am_bc[:], in_=attn_mask.rearrange("b l h -> (b l h)").partition_broadcast(P))
-            modalT = const.tile([P, L, 4], BF16)
-            with nc.allow_non_contiguous_dma(reason="256 eight-byte pieces, once"):
-                nc.sync.dma_start(
-                    out=modalT[:],
-                    in_=modal_attention.rearrange("l h d -> (l h d)").rearrange("(l p t) -> p l t", l=L, p=P, t=4),
-                )
-            wraw = mpool.tile([P, L, 4, DM], BF16, name="xm")
-            wsrc = W_O.rearrange("l h d n -> (l h d) n").rearrange("(l p t) n -> p l (t n)", l=L, p=P, t=4)
-            wdst = wraw[:].rearrange("p l t n -> p l (t n)")
-            a0 = load_attn(0, True)
-            m0 = load_mlp(0, True)
-            issue([a0[0], (wdst[:, 0, :], wsrc[:, 0, :]), a0[1], (wdst[:, 1, :], wsrc[:, 1, :])])
-            mm_bc = const.tile([P, B, M], BF16)
-            nc.scalar.dma_start(
-                out=mm_bc[:].rearrange("p b m -> p (b m)"), in_=mlp_mask.rearrange("b m -> (b m)").partition_broadcast(P)
-            )
-            rows = const.tile([P, DM], BF16)
-            nc.gpsimd.memset(rows[:], 0.0)
-            nc.scalar.dma_start(out=rows[0:M, :], in_=modal_mlp)
-            nc.scalar.dma_start(out=rows[M : M + L, :], in_=post_bias)
-            a1 = load_attn(1, True)
-            issue(a1)
-            issue([m0[1], m0[0], m0[2]])
-            o8 = const.tile([B, DM], BF16)
-            nc.sync.dma_start(out=o8[:], in_=orig_in[:, 0, :])
-            for b in range(2, AHEAD):
-                issue(load_attn(b, False))
-                issue(load_mlp(b - 1, False))
+        mrow = const.tile([P, NAM + B * M], BF16)
+        nc.vector.memset(mrow[:], 0.0)
+        rows = const.tile([P, DM], BF16)
+        nc.gpsimd.memset(rows[:], 0.0)
+        first_row = const.tile([P, P], BF16)
+        nc.vector.memset(first_row[:], 0.0)
+        nc.vector.memset(first_row[0:1, :], 1.0)
+        nc.sync.dma_start(out=mrow[0:1, 0:NAM], in_=attn_mask.rearrange("b l h -> (b l h)").unsqueeze(0))
+        nc.sync.dma_start(out=rows[R_ATT : R_ATT + L, :], in_=modal_attention.rearrange("l h d -> l (h d)"))
+        nc.scalar.dma_start(out=mrow[0:1, NAM:], in_=mlp_mask.rearrange("b m -> (b m)").unsqueeze(0))
+        nc.scalar.dma_start(out=rows[R_MLP : R_MLP + M, :], in_=modal_mlp)
+        nc.scalar.dma_start(out=rows[R_PB : R_PB + L, :], in_=post_bias)
+        wraw = mpool.tile([P, L, 4, DM], BF16, name="xm")
+        wsrc = W_O.rearrange("l h d n -> (l h d) n").rearrange("(l p t) n -> p l (t n)", l=L, p=P, t=4)
+        wdst = wraw[:].rearrange("p l t n -> p l (t n)")
+        a0 = load_attn(0, True)
+        m0 = load_mlp(0, True)
+        issue([a0[0], (wdst[:, 0, :], wsrc[:, 0, :]), a0[1], (wdst[:, 1, :], wsrc[:, 1, :])])
+        a1 = load_attn(1, True)
+        issue(a1)
+        issue([m0[1], m0[0], m0[2]])
+        o8 = const.tile([B, DM], BF16)
+        nc.sync.dma_start(out=o8[:], in_=orig_in[:, 0, :])
+        for b in range(2, AHEAD):
+            issue(load_attn(b, False))
+            issue(load_mlp(b - 1, False))
 
-            ident = const.tile([P, P], F32)
-            make_identity(nc, ident[:])
-            off = const.tile([P, H], F32)
-            nc.gpsimd.iota(off[:], pattern=[[-16, H]], base=0, channel_multiplier=1, allow_small_or_imprecise_dtypes=True)
-            warm = const.tile([P, 1], F32)
-            nc.scalar.activation(out=warm[:], in_=ident[:, 0:1], func=ACT.Identity, scale=1.0)
-            identb = const.tile([P, P], BF16)
-            make_identity(nc, identb[:])
+        identb = const.tile([P, P], BF16)
+        make_identity(nc, identb[:])
+        ident = const.tile([P, P], F32)
+        make_identity(nc, ident[:])
+        off = const.tile([P, H], F32)
+        nc.gpsimd.iota(off[:], pattern=[[-16, H]], base=0, channel_multiplier=1, allow_small_or_imprecise_dtypes=True)
+        warm = const.tile([P, 1], F32)
+        nc.scalar.activation(out=warm[:], in_=identb[:, 0:1], func=ACT.Identity, scale=1.0)
 
-            low = const.tile([P, H], F32)
-            nc.vector.tensor_scalar(out=low[:], in0=off[:], scalar1=15.0, scalar2=None, op0=ALU.is_le)
-            head = const.tile([P, H], F32)
-            nc.vector.scalar_tensor_tensor(out=head[:], in0=off[:], scalar=0.0, in1=low[:], op0=ALU.is_ge, op1=ALU.mult)
-            sel = const.tile([P, B * L, H], F32)
-            nc.vector.tensor_tensor(
-                out=sel[:],
-                in0=am_bc[:].rearrange("p (c h) -> p c h", h=H),
-                in1=head[:].unsqueeze(1).to_broadcast([P, B * L, H]),
-                op=ALU.mult,
-            )
-            scl = const.tile([P, B, L], F32)
-            nc.vector.reduce_sum(scl[:].rearrange("p b l -> p (b l)"), sel[:], axis=mybir.AxisListType.X)
-            om = const.tile([P, B * L], F32)
-            nc.vector.tensor_scalar(
-                out=om[:], in0=scl[:].rearrange("p b l -> p (b l)"), scalar1=-1.0, scalar2=1.0, op0=ALU.mult, op1=ALU.add
-            )
-            bia = const.tile([P, B, L, 4], F32)
-            nc.vector.tensor_tensor(
-                out=bia[:],
-                in0=om[:].rearrange("p (b l) -> p b l", l=L).unsqueeze(3).to_broadcast([P, B, L, 4]),
-                in1=modalT[:].unsqueeze(1).to_broadcast([P, B, L, 4]),
-                op=ALU.mult,
-            )
+        spread = psO.tile([P, NAM + B * M], F32, name="po")
+        nc.tensor.matmul(out=spread[:], lhsT=first_row[:], rhs=mrow[:], start=True, stop=True)
+        att = psZ.tile([P, 4, P], BF16, name="pz")
+        for t in range(4):
+            nc.tensor.transpose(out=att[:, t, :], in_=rows[:, t : 4 * P : 4], identity=identb[:])
+        low = const.tile([P, H], F32)
+        nc.vector.tensor_scalar(out=low[:], in0=off[:], scalar1=15.0, scalar2=None, op0=ALU.is_le)
+        head = const.tile([P, H], F32)
+        nc.vector.scalar_tensor_tensor(out=head[:], in0=off[:], scalar=0.0, in1=low[:], op0=ALU.is_ge, op1=ALU.mult)
+        sel = const.tile([P, B * L, H], F32)
+        nc.vector.tensor_tensor(
+            out=sel[:],
+            in0=spread[:, 0:NAM].rearrange("p (c h) -> p c h", h=H),
+            in1=head[:].unsqueeze(1).to_broadcast([P, B * L, H]),
+            op=ALU.mult,
+        )
+        mmf = const.tile([P, B, M], F32)
+        nc.vector.tensor_copy(out=mmf[:].rearrange("p b m -> p (b m)"), in_=spread[:, NAM:])
+        scl = const.tile([P, B, L], F32)
+        nc.vector.reduce_sum(scl[:].rearrange("p b l -> p (b l)"), sel[:], axis=mybir.AxisListType.X)
+        modalT = const.tile([P, L, 4], F32)
+        nc.vector.tensor_copy(out=modalT[:], in_=att[:, :, R_ATT : R_ATT + L].rearrange("p t l -> p l t"))
+        om = const.tile([P, B * L], F32)
+        nc.vector.tensor_scalar(
+            out=om[:], in0=scl[:].rearrange("p b l -> p (b l)"), scalar1=-1.0, scalar2=1.0, op0=ALU.mult, op1=ALU.add
+        )
+        bia = const.tile([P, B, L, 4], F32)
+        nc.vector.tensor_tensor(
+            out=bia[:],
+            in0=om[:].rearrange("p (b l) -> p b l", l=L).unsqueeze(3).to_broadcast([P, B, L, 4]),
+            in1=modalT[:].unsqueeze(1).to_broadcast([P, B, L, 4]),
+            op=ALU.mult,
+        )
+        diag = const.tile([P, B, P], BF16)
+        nc.gpsimd.tensor_tensor(
+            out=diag[:],
+            in0=identb[:].unsqueeze(1).to_broadcast([P, B, P]),
+            in1=mmf[:, :, 0:1].to_broadcast([P, B, P]),
+            op=ALU.mult,
+        )
+        cT = const.tile([P, NB, B], F32)
 
-            diag = const.tile([P, B, P], BF16)
-            nc.gpsimd.tensor_tensor(
-                out=diag[:],
-                in0=identb[:].unsqueeze(1).to_broadcast([P, B, P]),
-                in1=mm_bc[:, :, 0:1].to_broadcast([P, B, P]),
-                op=ALU.mult,
-            )
-            mmf = const.tile([P, B * M], F32)
-            cT = const.tile([P, NB, B], F32)
-
-            def const_columns():
-                pc = psO.tile([P, NB, P], BF16, name="po")
-                for nb in range(NB):
-                    nc.tensor.transpose(out=pc[:, nb, :], in_=rows[:, P * nb : P * nb + P], identity=identb[:])
-                rT = const.tile([P, NB, M + L], F32)
-                nc.vector.tensor_copy(out=rT[:], in_=pc[:, :, 0 : M + L])
-                omm = const.tile([P, B, M], F32)
-                nc.vector.tensor_scalar(out=omm[:], in0=mm_bc[:], scalar1=-1.0, scalar2=1.0, op0=ALU.mult, op1=ALU.add)
-                pbT = const.tile([P, NB], F32)
-                nc.vector.reduce_sum(pbT[:], rT[:, :, M : M + L], axis=mybir.AxisListType.X)
-                nc.vector.tensor_copy(out=mmf[:], in_=mm_bc[:].rearrange("p b m -> p (b m)"))
-                ct3 = const.tile([P, NB, B, M], F32)
-                for nb in range(NB):
-                    nc.vector.tensor_tensor(
-                        out=ct3[:, nb], in0=omm[:], in1=rT[:, nb : nb + 1, 0:M].to_broadcast([P, B, M]), op=ALU.mult
-                    )
-                ct1 = const.tile([P, NB, B], F32)
-                nc.vector.reduce_sum(ct1[:], ct3[:], axis=mybir.AxisListType.X)
+        def const_columns():
+            pc = psO.tile([P, NB, P], BF16, name="po")
+            for nb in range(NB):
+                nc.tensor.transpose(out=pc[:, nb, :], in_=rows[:, P * nb : P * nb + P], identity=identb[:])
+            rT = const.tile([P, NB, M + L], F32)
+            nc.vector.tensor_copy(out=rT[:], in_=pc[:, :, R_MLP : R_MLP + M + L])
+            omm = const.tile([P, B, M], F32)
+            nc.vector.tensor_scalar(out=omm[:], in0=mmf[:], scalar1=-1.0, scalar2=1.0, op0=ALU.mult, op1=ALU.add)
+            pbT = const.tile([P, NB], F32)
+            nc.vector.reduce_sum(pbT[:], rT[:, :, M : M + L], axis=mybir.AxisListType.X)
+            ct3 = const.tile([P, NB, B, M], F32)
+            for nb in range(NB):
                 nc.vector.tensor_tensor(
-                    out=cT[:], in0=ct1[:], in1=pbT[:].unsqueeze(2).to_broadcast([P, NB, B]), op=ALU.add
+                    out=ct3[:, nb], in0=omm[:], in1=rT[:, nb : nb + 1, 0:M].to_broadcast([P, B, M]), op=ALU.mult
                 )
+            ct1 = const.tile([P, NB, B], F32)
+            nc.vector.reduce_sum(ct1[:], ct3[:], axis=mybir.AxisListType.X)
+            nc.vector.tensor_tensor(
+                out=cT[:], in0=ct1[:], in1=pbT[:].unsqueeze(2).to_broadcast([P, NB, B]), op=ALU.add
+            )
 
-            wc = const.tile([P, L, DM], U32, align_bytes=64)
-            ws = const.tile([P, L, DM], U8, align_bytes=64)
+        wc = const.tile([P, L, DM], U32, align_bytes=64)
+        ws = const.tile([P, L, DM], U8, align_bytes=64)
 
-            wgs = {}
+        wgs = {}
 
-            def w_regroup(l):
-                grp = gpool.tile([P, DM, 4], BF16, align_bytes=64, name="grp")
-                wgs[l] = grp
-                interleave(nc.vector.tensor_copy, grp[:], wraw[:, l])
+        def w_regroup(l):
+            grp = gpool.tile([P, DM, 4], BF16, align_bytes=64, name="grp")
+            wgs[l] = grp
+            interleave(nc.vector.tensor_copy, grp[:], wraw[:, l])
 
-            def w_quant(l):
-                nc.vector.quantize_mx(
-                    out=wc[:, l, :].bitcast(FP8X4), scales=ws[:, l, :], in_=wgs[l][:].rearrange("p n t -> p (n t)")
-                )
+        def w_quant(l):
+            nc.vector.quantize_mx(
+                out=wc[:, l, :].bitcast(FP8X4), scales=ws[:, l, :], in_=wgs[l][:].rearrange("p n t -> p (n t)")
+            )
 
-            banks = {}
-            planes = {}
-            grps = {}
-            codes = {}
-            zs = {}
-            pos = {}
-            accs = {}
+        banks = {}
+        planes = {}
+        grps = {}
+        codes = {}
+        zs = {}
+        pos = {}
+        accs = {}
 
-            def turn(h):
-                b, l = divmod(h, L)
-                for u in range(2):
-                    pt = psT.tile([P, J, P], F32, name="pt")
-                    banks[h, u] = pt
-                    for j in range(J):
-                        nc.tensor.transpose(
-                            out=pt[:, j, :], in_=xas[b][:, l, j, :].bitcast(F32)[:, u : 2 * P : 2], identity=ident[:]
-                        )
-
-            def blend(h):
-                b, l = divmod(h, L)
-                pl = ppool.tile([P, 4, J * P], BF16, name="pl")
-                planes[h] = pl
-                for u in range(2):
-                    ptv = banks[h, u][:].rearrange("p j r -> p (j r)").bitcast(BF16).rearrange("p (c e) -> p c e", e=2)
-                    for e in range(2):
-                        nc.scalar.activation(
-                            out=pl[:, 2 * u + e, :],
-                            in_=ptv[:, :, e],
-                            func=ACT.Identity,
-                            bias=bia[:, b, l, 2 * u + e : 2 * u + e + 1],
-                            scale=scl[:, b, l : l + 1],
-                        )
-
-            def regroup(h, eng_copy):
-                grp = gpool.tile([P, J * P, 4], BF16, align_bytes=64, name="grp")
-                grps[h] = grp
-                interleave(eng_copy, grp[:], planes[h][:])
-
-            def quant(h):
-                ac = cpool.tile([P, J * P], U32, align_bytes=64, name="ac")
-                asc = cpool.tile([P, J * P], U8, align_bytes=64, name="asc")
-                nc.vector.quantize_mx(out=ac[:].bitcast(FP8X4), scales=asc[:], in_=grps[h][:].rearrange("p c t -> p (c t)"))
-                codes[h] = (ac, asc)
-
-            def mx(b, nb):
-                if nb == 0:
-                    z = zpool.tile([P, NB, J * P], F32, name="z")
-                    zs[b] = z
-                pz = psZ.tile([P, J * P], F32, name="pz")
-                for l in range(L):
-                    ac, asc = codes[L * b + l]
-                    nc.tensor.matmul_mx(
-                        out=pz[:],
-                        lhsT=wc[:, l, P * nb : P * nb + P].bitcast(FP8X4),
-                        lhsT_scale=ws[:, l, P * nb : P * nb + P],
-                        rhs=ac[:].bitcast(FP8X4),
-                        rhs_scale=asc[:],
-                        start=(l == 0),
-                        stop=(l == L - 1),
-                    )
-                nc.scalar.activation(out=zs[b][:, nb, :], in_=pz[:], func=ACT.Identity, bias=cT[:, nb, b : b + 1], scale=1.0)
-
-            def back(b, j):
-                on_pe = product_on_tensor(b, j)
-                po = psO.tile([P, NB, P], F32, name="po")
-                pos[b, j] = po
-                if on_pe:
-                    nc.tensor.matmul(
-                        out=po[:].rearrange("p a n -> p (a n)"), lhsT=diag[:, b, :], rhs=xms[b][:, 0, j, :], start=True, stop=False
-                    )
-                for nb in range(NB):
-                    nc.tensor.matmul(
-                        out=po[:, nb, :],
-                        lhsT=zs[b][:, nb, P * j : P * j + P],
-                        rhs=ident[:],
-                        start=not on_pe,
-                        stop=(not on_pe or nb == NB - 1),
-                        is_transpose=True,
+        def turn(h):
+            b, l = divmod(h, L)
+            for u in range(2):
+                pt = psT.tile([P, J, P], F32, name="pt")
+                banks[h, u] = pt
+                for j in range(J):
+                    nc.tensor.transpose(
+                        out=pt[:, j, :], in_=xas[b][:, l, j, :].bitcast(F32)[:, u : 2 * P : 2], identity=ident[:]
                     )
 
-            def term(b, m, acc, js, other):
-                nc.vector.scalar_tensor_tensor(
-                    out=acc,
-                    in0=xms[b][:, m, js, :],
-                    scalar=mmf[:, M * b + m : M * b + m + 1],
-                    in1=other,
-                    op0=ALU.mult,
-                    op1=ALU.add,
+        def blend(h):
+            b, l = divmod(h, L)
+            pl = ppool.tile([P, 4, J * P], BF16, name="pl")
+            planes[h] = pl
+            for u in range(2):
+                ptv = banks[h, u][:].rearrange("p j r -> p (j r)").bitcast(BF16).rearrange("p (c e) -> p c e", e=2)
+                for e in range(2):
+                    nc.scalar.activation(
+                        out=pl[:, 2 * u + e, :],
+                        in_=ptv[:, :, e],
+                        func=ACT.Identity,
+                        bias=bia[:, b, l, 2 * u + e : 2 * u + e + 1],
+                        scale=scl[:, b, l : l + 1],
+                    )
+
+        def regroup(h, eng_copy):
+            grp = gpool.tile([P, J * P, 4], BF16, align_bytes=64, name="grp")
+            grps[h] = grp
+            interleave(eng_copy, grp[:], planes[h][:])
+
+        def quant(h):
+            ac = cpool.tile([P, J * P], U32, align_bytes=64, name="ac")
+            asc = cpool.tile([P, J * P], U8, align_bytes=64, name="asc")
+            nc.vector.quantize_mx(out=ac[:].bitcast(FP8X4), scales=asc[:], in_=grps[h][:].rearrange("p c t -> p (c t)"))
+            codes[h] = (ac, asc)
+
+        def mx(b, nb):
+            if nb == 0:
+                z = zpool.tile([P, NB, J * P], F32, name="z")
+                zs[b] = z
+            pz = psZ.tile([P, J * P], F32, name="pz")
+            for l in range(L):
+                ac, asc = codes[L * b + l]
+                nc.tensor.matmul_mx(
+                    out=pz[:],
+                    lhsT=wc[:, l, P * nb : P * nb + P].bitcast(FP8X4),
+                    lhsT_scale=ws[:, l, P * nb : P * nb + P],
+                    rhs=ac[:].bitcast(FP8X4),
+                    rhs_scale=asc[:],
+                    start=(l == 0),
+                    stop=(l == L - 1),
+                )
+            nc.scalar.activation(out=zs[b][:, nb, :], in_=pz[:], func=ACT.Identity, bias=cT[:, nb, b : b + 1], scale=1.0)
+
+        def back(b, j):
+            on_pe = product_on_tensor(b, j)
+            po = psO.tile([P, NB, P], F32, name="po")
+            pos[b, j] = po
+            if on_pe:
+                nc.tensor.matmul(
+                    out=po[:].rearrange("p a n -> p (a n)"), lhsT=diag[:, b, :], rhs=xms[b][:, 0, j, :], start=True, stop=False
+                )
+            for nb in range(NB):
+                nc.tensor.matmul(
+                    out=po[:, nb, :],
+                    lhsT=zs[b][:, nb, P * j : P * j + P],
+                    rhs=ident[:],
+                    start=not on_pe,
+                    stop=(not on_pe or nb == NB - 1),
+                    is_transpose=True,
                 )
 
-            def first_terms(b, j):
-                half, jj = divmod(j, 2)
-                if jj == 0:
-                    acc = opool.tile([P, 2, DM], F32, name="acc")
-                    accs[b, half] = acc
-                acc = accs[b, half][:, jj : jj + 1, :]
-                js = slice(j, j + 1)
-                term(b, 1, acc, js, pos[b, j][:].rearrange("p a n -> p (a n)").unsqueeze(1))
-                if not product_on_tensor(b, j):
-                    term(b, 0, acc, js, acc)
+        def term(b, m, acc, js, other):
+            nc.vector.scalar_tensor_tensor(
+                out=acc,
+                in0=xms[b][:, m, js, :],
+                scalar=mmf[:, b, m : m + 1],
+                in1=other,
+                op0=ALU.mult,
+                op1=ALU.add,
+            )
 
-            def last_term(b, half):
-                acc = accs[b, half]
-                js = slice(2 * half, 2 * half + 2)
+        def early_terms(half):
+            acc = opool.tile([P, 2, DM], F32, name="acc")
+            accs[0, half] = acc
+            js = slice(2 * half, 2 * half + 2)
+            nc.vector.tensor_scalar(out=acc[:], in0=xms[0][:, 0, js, :], scalar1=mmf[:, 0, 0:1], scalar2=None, op0=ALU.mult)
+            for m in range(1, M):
+                term(0, m, acc[:], js, acc[:])
+
+        def first_terms(b, j):
+            half, jj = divmod(j, 2)
+            if jj == 0 and b > 0:
+                acc = opool.tile([P, 2, DM], F32, name="acc")
+                accs[b, half] = acc
+            acc = accs[b, half][:, jj : jj + 1, :]
+            js = slice(j, j + 1)
+            po = pos[b, j][:].rearrange("p a n -> p (a n)").unsqueeze(1)
+            if b == 0:
+                nc.vector.tensor_tensor(out=acc, in0=acc, in1=po, op=ALU.add)
+                return
+            term(b, 1, acc, js, po)
+            if not product_on_tensor(b, j):
+                term(b, 0, acc, js, acc)
+
+        def last_term(b, half):
+            acc = accs[b, half]
+            js = slice(2 * half, 2 * half + 2)
+            if b > 0:
                 term(b, 2, acc[:], js, acc[:])
-                dst = out[b, 1:POS, :].rearrange("(p j) n -> p j n", j=J)
-                nc.sync.dma_start(out=dst[:, js, :], in_=acc[:])
+            dst = out[b, 1:POS, :].rearrange("(p j) n -> p j n", j=J)
+            nc.sync.dma_start(out=dst[:, js, :], in_=acc[:])
 
-            turn(0)
-            blend(0)
-            w_regroup(0)
-            const_columns()
-            w_quant(0)
-            o8f = const.tile([B, DM], F32)
-            nc.gpsimd.tensor_copy(out=o8f[:], in_=o8[:])
+        turn(0)
+        blend(0)
+        w_regroup(0)
+        const_columns()
+        w_quant(0)
+        o8f = const.tile([B, DM], F32)
+        nc.gpsimd.tensor_copy(out=o8f[:], in_=o8[:])
 
         for h in range(L * B + 5 + LAG):
             hv = h - LAG
@@ -336,6 +353,8 @@ def tile_edgepruner_t_kernel(
                 quant(hv)
             if hv == 0:
                 w_quant(1)
+            if hv in (2, 3):
+                early_terms(hv - 2)
             if 0 <= bd < B:
                 for j in (2 * half, 2 * half + 1):
                     first_terms(bd, j)

@@ -14,13 +14,13 @@ ACT = mybir.ActivationFunctionType
 L, B, POS, H, DH, DM = 2, 8, 513, 8, 64, 512
 M = 3
 NAM = B * L * H
-R_ATT, R_MLP, R_PB = 0, L, L + M
+R_MLP, R_PB = 0, M
 P = 128
 J = 4
 NB = DM // P
 R = POS - 1
-AHEAD = 5
-LAG = 0
+AHEAD = 4
+V_COLUMNS = 160
 KL = H * DH
 
 FLOPS = 2 * B * R * L * KL * DM
@@ -34,12 +34,8 @@ def interleave(eng_copy, dst, src):
     )
 
 
-def interleave_on_vector(h):
-    return h < 2 or h % 8 in (0, 1, 3, 4, 5, 7)
-
-
 def product_on_tensor(b, j):
-    return b > 0 and (j < 3 or b >= 4)
+    return j < 3 or b == B - 1
 
 
 def tile_edgepruner_t_kernel(
@@ -51,13 +47,13 @@ def tile_edgepruner_t_kernel(
         apool = ctx.enter_context(tc.tile_pool(name="apool", bufs=5))
         mpool = ctx.enter_context(tc.tile_pool(name="mpool", bufs=7))
         opool = ctx.enter_context(tc.tile_pool(name="opool", bufs=5))
-        zpool = ctx.enter_context(tc.tile_pool(name="zpool", bufs=2))
+        upool = ctx.enter_context(tc.tile_pool(name="upool", bufs=3))
         ppool = ctx.enter_context(tc.tile_pool(name="ppool", bufs=3))
         gpool = ctx.enter_context(tc.tile_pool(name="gpool", bufs=4))
         cpool = ctx.enter_context(tc.tile_pool(name="cpool", bufs=5))
         psT = ctx.enter_context(tc.psum_pool(name="psT", bufs=3))
-        psZ = ctx.enter_context(tc.psum_pool(name="psZ", bufs=2))
-        psO = ctx.enter_context(tc.psum_pool(name="psO", bufs=3))
+        psP = ctx.enter_context(tc.psum_pool(name="psP", bufs=2))
+        psM = ctx.enter_context(tc.psum_pool(name="psM", bufs=3))
         ctx.enter_context(tc.manual_schedule())
 
         xas = {}
@@ -87,22 +83,25 @@ def tile_edgepruner_t_kernel(
 
         mrow = const.tile([P, NAM + B * M], BF16)
         nc.vector.memset(mrow[:], 0.0)
+        arow = const.tile([P, DM], BF16)
+        nc.gpsimd.memset(arow[:], 0.0)
         rows = const.tile([P, DM], BF16)
         nc.gpsimd.memset(rows[:], 0.0)
         first_row = const.tile([P, P], BF16)
         nc.vector.memset(first_row[:], 0.0)
         nc.vector.memset(first_row[0:1, :], 1.0)
         nc.sync.dma_start(out=mrow[0:1, 0:NAM], in_=attn_mask.rearrange("b l h -> (b l h)").unsqueeze(0))
-        nc.sync.dma_start(out=rows[R_ATT : R_ATT + L, :], in_=modal_attention.rearrange("l h d -> l (h d)"))
-        nc.scalar.dma_start(out=mrow[0:1, NAM:], in_=mlp_mask.rearrange("b m -> (b m)").unsqueeze(0))
-        nc.scalar.dma_start(out=rows[R_MLP : R_MLP + M, :], in_=modal_mlp)
-        nc.scalar.dma_start(out=rows[R_PB : R_PB + L, :], in_=post_bias)
+        nc.sync.dma_start(out=arow[0:L, :], in_=modal_attention.rearrange("l h d -> l (h d)"))
         wraw = mpool.tile([P, L, 4, DM], BF16, name="xm")
         wsrc = W_O.rearrange("l h d n -> (l h d) n").rearrange("(l p t) n -> p l (t n)", l=L, p=P, t=4)
         wdst = wraw[:].rearrange("p l t n -> p l (t n)")
         a0 = load_attn(0, True)
         m0 = load_mlp(0, True)
-        issue([a0[0], (wdst[:, 0, :], wsrc[:, 0, :]), a0[1], (wdst[:, 1, :], wsrc[:, 1, :])])
+        nc.scalar.dma_start(out=a0[0][0], in_=a0[0][1])
+        nc.scalar.dma_start(out=mrow[0:1, NAM:], in_=mlp_mask.rearrange("b m -> (b m)").unsqueeze(0))
+        nc.scalar.dma_start(out=rows[R_MLP : R_MLP + M, :], in_=modal_mlp)
+        nc.scalar.dma_start(out=rows[R_PB : R_PB + L, :], in_=post_bias)
+        issue([(wdst[:, 0, :], wsrc[:, 0, :]), a0[1], (wdst[:, 1, :], wsrc[:, 1, :])])
         a1 = load_attn(1, True)
         issue(a1)
         issue([m0[1], m0[0], m0[2]])
@@ -121,11 +120,11 @@ def tile_edgepruner_t_kernel(
         warm = const.tile([P, 1], F32)
         nc.scalar.activation(out=warm[:], in_=identb[:, 0:1], func=ACT.Identity, scale=1.0)
 
-        spread = psO.tile([P, NAM + B * M], F32, name="po")
-        nc.tensor.matmul(out=spread[:], lhsT=first_row[:], rhs=mrow[:], start=True, stop=True)
-        att = psZ.tile([P, 4, P], BF16, name="pz")
+        spread = psM.tile([P, NAM], F32, name="pm")
+        nc.tensor.matmul(out=spread[:], lhsT=first_row[:], rhs=mrow[:, 0:NAM], start=True, stop=True)
+        att = psP.tile([P, 4, P], BF16, name="pp")
         for t in range(4):
-            nc.tensor.transpose(out=att[:, t, :], in_=rows[:, t : 4 * P : 4], identity=identb[:])
+            nc.tensor.transpose(out=att[:, t, :], in_=arow[:, t : 4 * P : 4], identity=identb[:])
         low = const.tile([P, H], F32)
         nc.vector.tensor_scalar(out=low[:], in0=off[:], scalar1=15.0, scalar2=None, op0=ALU.is_le)
         head = const.tile([P, H], F32)
@@ -133,16 +132,14 @@ def tile_edgepruner_t_kernel(
         sel = const.tile([P, B * L, H], F32)
         nc.vector.tensor_tensor(
             out=sel[:],
-            in0=spread[:, 0:NAM].rearrange("p (c h) -> p c h", h=H),
+            in0=spread[:].rearrange("p (c h) -> p c h", h=H),
             in1=head[:].unsqueeze(1).to_broadcast([P, B * L, H]),
             op=ALU.mult,
         )
-        mmf = const.tile([P, B, M], F32)
-        nc.vector.tensor_copy(out=mmf[:].rearrange("p b m -> p (b m)"), in_=spread[:, NAM:])
         scl = const.tile([P, B, L], F32)
         nc.vector.reduce_sum(scl[:].rearrange("p b l -> p (b l)"), sel[:], axis=mybir.AxisListType.X)
         modalT = const.tile([P, L, 4], F32)
-        nc.vector.tensor_copy(out=modalT[:], in_=att[:, :, R_ATT : R_ATT + L].rearrange("p t l -> p l t"))
+        nc.vector.tensor_copy(out=modalT[:], in_=att[:, :, 0:L].rearrange("p t l -> p l t"))
         om = const.tile([P, B * L], F32)
         nc.vector.tensor_scalar(
             out=om[:], in0=scl[:].rearrange("p b l -> p (b l)"), scalar1=-1.0, scalar2=1.0, op0=ALU.mult, op1=ALU.add
@@ -154,17 +151,21 @@ def tile_edgepruner_t_kernel(
             in1=modalT[:].unsqueeze(1).to_broadcast([P, B, L, 4]),
             op=ALU.mult,
         )
+        mmf = const.tile([P, B, M], F32)
         diag = const.tile([P, B, P], BF16)
-        nc.gpsimd.tensor_tensor(
-            out=diag[:],
-            in0=identb[:].unsqueeze(1).to_broadcast([P, B, P]),
-            in1=mmf[:, :, 0:1].to_broadcast([P, B, P]),
-            op=ALU.mult,
-        )
         cT = const.tile([P, NB, B], F32)
 
         def const_columns():
-            pc = psO.tile([P, NB, P], BF16, name="po")
+            spread_m = psM.tile([P, B * M], F32, name="pm")
+            nc.tensor.matmul(out=spread_m[:], lhsT=first_row[:], rhs=mrow[:, NAM:], start=True, stop=True)
+            nc.vector.tensor_copy(out=mmf[:].rearrange("p b m -> p (b m)"), in_=spread_m[:])
+            nc.gpsimd.tensor_tensor(
+                out=diag[:],
+                in0=identb[:].unsqueeze(1).to_broadcast([P, B, P]),
+                in1=mmf[:, :, 0:1].to_broadcast([P, B, P]),
+                op=ALU.mult,
+            )
+            pc = psM.tile([P, NB, P], BF16, name="pm")
             for nb in range(NB):
                 nc.tensor.transpose(out=pc[:, nb, :], in_=rows[:, P * nb : P * nb + P], identity=identb[:])
             rT = const.tile([P, NB, M + L], F32)
@@ -203,7 +204,8 @@ def tile_edgepruner_t_kernel(
         planes = {}
         grps = {}
         codes = {}
-        zs = {}
+        pms = {}
+        ups = {}
         pos = {}
         accs = {}
 
@@ -232,10 +234,15 @@ def tile_edgepruner_t_kernel(
                         scale=scl[:, b, l : l + 1],
                     )
 
-        def regroup(h, eng_copy):
+        def regroup_scalar(h):
             grp = gpool.tile([P, J * P, 4], BF16, align_bytes=64, name="grp")
             grps[h] = grp
-            interleave(eng_copy, grp[:], planes[h][:])
+            if h >= 2:
+                interleave(nc.scalar.copy, grp[:, V_COLUMNS:], planes[h][:, :, V_COLUMNS:])
+
+        def regroup_vector(h):
+            cols = V_COLUMNS if h >= 2 else J * P
+            interleave(nc.vector.tensor_copy, grps[h][:, 0:cols], planes[h][:, :, 0:cols])
 
         def quant(h):
             ac = cpool.tile([P, J * P], U32, align_bytes=64, name="ac")
@@ -243,27 +250,9 @@ def tile_edgepruner_t_kernel(
             nc.vector.quantize_mx(out=ac[:].bitcast(FP8X4), scales=asc[:], in_=grps[h][:].rearrange("p c t -> p (c t)"))
             codes[h] = (ac, asc)
 
-        def mx(b, nb):
-            if nb == 0:
-                z = zpool.tile([P, NB, J * P], F32, name="z")
-                zs[b] = z
-            pz = psZ.tile([P, J * P], F32, name="pz")
-            for l in range(L):
-                ac, asc = codes[L * b + l]
-                nc.tensor.matmul_mx(
-                    out=pz[:],
-                    lhsT=wc[:, l, P * nb : P * nb + P].bitcast(FP8X4),
-                    lhsT_scale=ws[:, l, P * nb : P * nb + P],
-                    rhs=ac[:].bitcast(FP8X4),
-                    rhs_scale=asc[:],
-                    start=(l == 0),
-                    stop=(l == L - 1),
-                )
-            nc.scalar.activation(out=zs[b][:, nb, :], in_=pz[:], func=ACT.Identity, bias=cT[:, nb, b : b + 1], scale=1.0)
-
-        def back(b, j):
+        def plain(b, j):
             on_pe = product_on_tensor(b, j)
-            po = psO.tile([P, NB, P], F32, name="po")
+            po = psP.tile([P, NB, P], F32, name="pp")
             pos[b, j] = po
             if on_pe:
                 nc.tensor.matmul(
@@ -272,92 +261,94 @@ def tile_edgepruner_t_kernel(
             for nb in range(NB):
                 nc.tensor.matmul(
                     out=po[:, nb, :],
-                    lhsT=zs[b][:, nb, P * j : P * j + P],
+                    lhsT=cT[:, nb, b : b + 1].to_broadcast([P, P]),
                     rhs=ident[:],
                     start=not on_pe,
                     stop=(not on_pe or nb == NB - 1),
                     is_transpose=True,
                 )
 
-        def term(b, m, acc, js, other):
+        def mx(b, j):
+            pm = psM.tile([P, DM], F32, name="pm")
+            pms[b, j] = pm
+            for l in range(L):
+                ac, asc = codes[L * b + l]
+                nc.tensor.matmul_mx(
+                    out=pm[:],
+                    lhsT=ac[:, P * j : P * j + P].bitcast(FP8X4),
+                    lhsT_scale=asc[:, P * j : P * j + P],
+                    rhs=wc[:, l, :].bitcast(FP8X4),
+                    rhs_scale=ws[:, l, :],
+                    start=(l == 0),
+                    stop=(l == L - 1),
+                )
+
+        def term(out_, b, m, j, other):
             nc.vector.scalar_tensor_tensor(
-                out=acc,
-                in0=xms[b][:, m, js, :],
-                scalar=mmf[:, b, m : m + 1],
-                in1=other,
-                op0=ALU.mult,
-                op1=ALU.add,
+                out=out_, in0=xms[b][:, m, j, :], scalar=mmf[:, b, m : m + 1], in1=other, op0=ALU.mult, op1=ALU.add
             )
 
-        def early_terms(half):
-            acc = opool.tile([P, 2, DM], F32, name="acc")
-            accs[0, half] = acc
-            js = slice(2 * half, 2 * half + 2)
-            nc.vector.tensor_scalar(out=acc[:], in0=xms[0][:, 0, js, :], scalar1=mmf[:, 0, 0:1], scalar2=None, op0=ALU.mult)
-            for m in range(1, M):
-                term(0, m, acc[:], js, acc[:])
-
-        def first_terms(b, j):
+        def upper(b, j):
             half, jj = divmod(j, 2)
-            if jj == 0 and b > 0:
+            if jj == 0:
+                up = upool.tile([P, 2, DM], F32, name="up")
+                ups[b, half] = up
+            term(ups[b, half][:, jj, :], b, 2, j, pos[b, j][:].rearrange("p a n -> p (a n)"))
+
+        def middle(b, j):
+            if not product_on_tensor(b, j):
+                up = ups[b, j // 2][:, j % 2, :]
+                term(up, b, 0, j, up)
+
+        def lower(b, j):
+            half, jj = divmod(j, 2)
+            if jj == 0:
                 acc = opool.tile([P, 2, DM], F32, name="acc")
                 accs[b, half] = acc
-            acc = accs[b, half][:, jj : jj + 1, :]
-            js = slice(j, j + 1)
-            po = pos[b, j][:].rearrange("p a n -> p (a n)").unsqueeze(1)
-            if b == 0:
-                nc.vector.tensor_tensor(out=acc, in0=acc, in1=po, op=ALU.add)
-                return
-            term(b, 1, acc, js, po)
-            if not product_on_tensor(b, j):
-                term(b, 0, acc, js, acc)
+            term(accs[b, half][:, jj, :], b, 1, j, pms[b, j][:])
 
-        def last_term(b, half):
+        def finish(b, half):
             acc = accs[b, half]
-            js = slice(2 * half, 2 * half + 2)
-            if b > 0:
-                term(b, 2, acc[:], js, acc[:])
+            nc.gpsimd.tensor_tensor(out=acc[:], in0=acc[:], in1=ups[b, half][:], op=ALU.add)
             dst = out[b, 1:POS, :].rearrange("(p j) n -> p j n", j=J)
-            nc.sync.dma_start(out=dst[:, js, :], in_=acc[:])
+            nc.sync.dma_start(out=dst[:, 2 * half : 2 * half + 2, :], in_=acc[:])
 
         turn(0)
         blend(0)
+        regroup_scalar(0)
         w_regroup(0)
         const_columns()
         w_quant(0)
         o8f = const.tile([B, DM], F32)
         nc.gpsimd.tensor_copy(out=o8f[:], in_=o8[:])
 
-        for h in range(L * B + 5 + LAG):
-            hv = h - LAG
-            bx, half = divmod(hv - 2, 2)
-            bd = bx - 1
+        for h in range(L * B + 3):
+            bx, half = divmod(h - 2, 2)
+            js = (2 * half, 2 * half + 1) if 0 <= bx < B else ()
             if h + 1 < L * B:
                 turn(h + 1)
                 blend(h + 1)
-            if 0 <= bx < B:
-                for nb in (2 * half, 2 * half + 1):
-                    mx(bx, nb)
-            if 0 <= bd < B:
-                for j in (2 * half, 2 * half + 1):
-                    back(bd, j)
-            if h + 1 < L * B and not interleave_on_vector(h + 1):
-                regroup(h + 1, nc.scalar.copy)
-            if 0 <= hv < L * B and interleave_on_vector(hv):
-                regroup(hv, nc.vector.tensor_copy)
-            if hv == 0:
+                regroup_scalar(h + 1)
+            for j in js:
+                plain(bx, j)
+            for j in js:
+                mx(bx, j)
+            if h < L * B:
+                regroup_vector(h)
+            if h == 0:
                 w_regroup(1)
-            if hv - 5 >= 0:
-                last_term(*divmod(hv - 5, 2))
-            if 0 <= hv < L * B:
-                quant(hv)
-            if hv == 0:
+            for j in js:
+                upper(bx, j)
+            if h < L * B:
+                quant(h)
+            if h == 0:
                 w_quant(1)
-            if hv in (2, 3):
-                early_terms(hv - 2)
-            if 0 <= bd < B:
-                for j in (2 * half, 2 * half + 1):
-                    first_terms(bd, j)
+            for j in js:
+                middle(bx, j)
+            for j in js:
+                lower(bx, j)
+            if 0 <= h - 3 < L * B:
+                finish(*divmod(h - 3, 2))
             if h % 2 == 1:
                 b = h // 2
                 if b + AHEAD < B:

@@ -309,7 +309,12 @@ def tile_edgepruner_t_kernel(
 
         def finish(b, half):
             acc = accs[b, half]
-            nc.gpsimd.tensor_tensor(out=acc[:], in0=acc[:], in1=ups[b, half][:], op=ALU.add)
+            for jj in range(2):
+                for c in range(0, DM, DM // 2):
+                    piece = acc[:, jj, c : c + DM // 2]
+                    nc.gpsimd.tensor_tensor(
+                        out=piece, in0=piece, in1=ups[b, half][:, jj, c : c + DM // 2], op=ALU.add
+                    )
             dst = out[b, 1:POS, :].rearrange("(p j) n -> p j n", j=J)
             nc.sync.dma_start(out=dst[:, 2 * half : 2 * half + 2, :], in_=acc[:])
 

@@ -20,7 +20,7 @@ J = 4
 NB = DM // P
 R = POS - 1
 AHEAD = 4
-V_COLUMNS = 160
+V_COLUMNS = 224
 KL = H * DH
 
 FLOPS = 2 * B * R * L * KL * DM
@@ -32,6 +32,10 @@ def interleave(eng_copy, dst, src):
         out=dst.rearrange("p (c i) t -> p c t i", i=4),
         in_=src.rearrange("p t (c i) -> p c t i", i=4),
     )
+
+
+def summed_on_vector(b):
+    return b == B - 1
 
 
 def product_on_tensor(b, j):
@@ -296,18 +300,28 @@ def tile_edgepruner_t_kernel(
             term(ups[b, half][:, jj, :], b, 2, j, pos[b, j][:].rearrange("p a n -> p (a n)"))
 
         def middle(b, j):
+            up = ups[b, j // 2][:, j % 2, :]
             if not product_on_tensor(b, j):
-                up = ups[b, j // 2][:, j % 2, :]
                 term(up, b, 0, j, up)
+            if summed_on_vector(b):
+                term(up, b, 1, j, up)
 
         def lower(b, j):
             half, jj = divmod(j, 2)
+            if summed_on_vector(b):
+                up = ups[b, half][:, jj, :]
+                nc.vector.tensor_tensor(out=up, in0=up, in1=pms[b, j][:], op=ALU.add)
+                dst = out[b, 1:POS, :].rearrange("(p j) n -> p j n", j=J)
+                nc.sync.dma_start(out=dst[:, j, :], in_=up)
+                return
             if jj == 0:
                 acc = opool.tile([P, 2, DM], F32, name="acc")
                 accs[b, half] = acc
             term(accs[b, half][:, jj, :], b, 1, j, pms[b, j][:])
 
         def finish(b, half):
+            if summed_on_vector(b):
+                return
             acc = accs[b, half]
             for jj in range(2):
                 for c in range(0, DM, DM // 2):

@@ -20,7 +20,8 @@ J = 4
 NB = DM // P
 R = POS - 1
 AHEAD = 4
-V_COLUMNS = 224
+FIRST_SPLIT = 1
+V_COLUMNS = 128
 KL = H * DH
 
 FLOPS = 2 * B * R * L * KL * DM
@@ -50,8 +51,8 @@ def tile_edgepruner_t_kernel(
         const = ctx.enter_context(tc.tile_pool(name="const", bufs=1))
         apool = ctx.enter_context(tc.tile_pool(name="apool", bufs=5))
         mpool = ctx.enter_context(tc.tile_pool(name="mpool", bufs=7))
-        opool = ctx.enter_context(tc.tile_pool(name="opool", bufs=5))
-        upool = ctx.enter_context(tc.tile_pool(name="upool", bufs=3))
+        opool = ctx.enter_context(tc.tile_pool(name="opool", bufs=4))
+        upool = ctx.enter_context(tc.tile_pool(name="upool", bufs=5))
         ppool = ctx.enter_context(tc.tile_pool(name="ppool", bufs=3))
         gpool = ctx.enter_context(tc.tile_pool(name="gpool", bufs=4))
         cpool = ctx.enter_context(tc.tile_pool(name="cpool", bufs=5))
@@ -241,11 +242,11 @@ def tile_edgepruner_t_kernel(
         def regroup_scalar(h):
             grp = gpool.tile([P, J * P, 4], BF16, align_bytes=64, name="grp")
             grps[h] = grp
-            if h >= 2:
+            if h >= FIRST_SPLIT:
                 interleave(nc.scalar.copy, grp[:, V_COLUMNS:], planes[h][:, :, V_COLUMNS:])
 
         def regroup_vector(h):
-            cols = V_COLUMNS if h >= 2 else J * P
+            cols = V_COLUMNS if h >= FIRST_SPLIT else J * P
             interleave(nc.vector.tensor_copy, grps[h][:, 0:cols], planes[h][:, :, 0:cols])
 
         def quant(h):
@@ -348,24 +349,33 @@ def tile_edgepruner_t_kernel(
                 turn(h + 1)
                 blend(h + 1)
                 regroup_scalar(h + 1)
-            for j in js:
-                plain(bx, j)
+            tiles = [(bx, j) for j in js if bx < B - 1]
+            for b, j in tiles:
+                plain(b, j)
             for j in js:
                 mx(bx, j)
             if h < L * B:
                 regroup_vector(h)
             if h == 0:
                 w_regroup(1)
-            for j in js:
-                upper(bx, j)
+            for b, j in tiles:
+                upper(b, j)
             if h < L * B:
                 quant(h)
             if h == 0:
                 w_quant(1)
-            for j in js:
-                middle(bx, j)
+            for b, j in tiles:
+                middle(b, j)
             for j in js:
                 lower(bx, j)
+            if L * (B - 1) <= h < L * B:
+                last = [(B - 1, j) for j in js]
+                for b, j in last:
+                    plain(b, j)
+                for b, j in last:
+                    upper(b, j)
+                for b, j in last:
+                    middle(b, j)
             if 0 <= h - 3 < L * B:
                 finish(*divmod(h - 3, 2))
             if h % 2 == 1:

@@ -21,7 +21,8 @@ NB = DM // P
 R = POS - 1
 AHEAD = 4
 FIRST_SPLIT = 1
-V_COLUMNS = 128
+PIECE = 256
+V_COLUMNS = 160
 KL = H * DH
 
 FLOPS = 2 * B * R * L * KL * DM
@@ -51,7 +52,7 @@ def tile_edgepruner_t_kernel(
         const = ctx.enter_context(tc.tile_pool(name="const", bufs=1))
         apool = ctx.enter_context(tc.tile_pool(name="apool", bufs=5))
         mpool = ctx.enter_context(tc.tile_pool(name="mpool", bufs=7))
-        opool = ctx.enter_context(tc.tile_pool(name="opool", bufs=4))
+        opool = ctx.enter_context(tc.tile_pool(name="opool", bufs=5))
         upool = ctx.enter_context(tc.tile_pool(name="upool", bufs=5))
         ppool = ctx.enter_context(tc.tile_pool(name="ppool", bufs=3))
         gpool = ctx.enter_context(tc.tile_pool(name="gpool", bufs=4))
@@ -325,11 +326,9 @@ def tile_edgepruner_t_kernel(
                 return
             acc = accs[b, half]
             for jj in range(2):
-                for c in range(0, DM, DM // 2):
-                    piece = acc[:, jj, c : c + DM // 2]
-                    nc.gpsimd.tensor_tensor(
-                        out=piece, in0=piece, in1=ups[b, half][:, jj, c : c + DM // 2], op=ALU.add
-                    )
+                for c in range(0, DM, PIECE):
+                    piece = acc[:, jj, c : c + PIECE]
+                    nc.gpsimd.tensor_tensor(out=piece, in0=piece, in1=ups[b, half][:, jj, c : c + PIECE], op=ALU.add)
             dst = out[b, 1:POS, :].rearrange("(p j) n -> p j n", j=J)
             nc.sync.dma_start(out=dst[:, 2 * half : 2 * half + 2, :], in_=acc[:])
 
@@ -349,33 +348,26 @@ def tile_edgepruner_t_kernel(
                 turn(h + 1)
                 blend(h + 1)
                 regroup_scalar(h + 1)
-            tiles = [(bx, j) for j in js if bx < B - 1]
-            for b, j in tiles:
-                plain(b, j)
             for j in js:
                 mx(bx, j)
+            if 1 <= h <= L * B:
+                b, first = divmod(2 * (h - 1), J)
+                for j in (first, first + 1):
+                    plain(b, j)
             if h < L * B:
                 regroup_vector(h)
             if h == 0:
                 w_regroup(1)
-            for b, j in tiles:
-                upper(b, j)
+            for j in js:
+                upper(bx, j)
             if h < L * B:
                 quant(h)
             if h == 0:
                 w_quant(1)
-            for b, j in tiles:
-                middle(b, j)
+            for j in js:
+                middle(bx, j)
             for j in js:
                 lower(bx, j)
-            if L * (B - 1) <= h < L * B:
-                last = [(B - 1, j) for j in js]
-                for b, j in last:
-                    plain(b, j)
-                for b, j in last:
-                    upper(b, j)
-                for b, j in last:
-                    middle(b, j)
             if 0 <= h - 3 < L * B:
                 finish(*divmod(h - 3, 2))
             if h % 2 == 1:

from contextlib import ExitStack

import concourse.mybir as mybir
from concourse.masks import make_identity

F32 = mybir.dt.float32
BF16 = mybir.dt.bfloat16
U32 = mybir.dt.uint32
U8 = mybir.dt.uint8
FP8X4 = mybir.dt.float8_e4m3fn_x4
ALU = mybir.AluOpType
ACT = mybir.ActivationFunctionType

L, B, POS, H, DH, DM = 2, 8, 513, 8, 64, 512
M = 3
NAM = B * L * H
R_MLP, R_PB = 0, M
P = 128
J = 4
NB = DM // P
R = POS - 1
AHEAD = 4
FIRST_SPLIT = 1
PIECE = 256
V_COLUMNS = 160
KL = H * DH

FLOPS = 2 * B * R * L * KL * DM
BYTES = 2 * (L * B * R * KL + M * B * R * DM + L * KL * DM) + 4 * B * POS * DM


def interleave(eng_copy, dst, src):
    eng_copy(
        out=dst.rearrange("p (c i) t -> p c t i", i=4),
        in_=src.rearrange("p t (c i) -> p c t i", i=4),
    )


def summed_on_vector(b):
    return b == B - 1


def product_on_tensor(b, j):
    return j < 3 or b == B - 1


def tile_edgepruner_t_kernel(
    tc, attn_cache, mlp_cache, mlp_mask, attn_mask, modal_attention, modal_mlp, W_O, post_bias, orig_in, out
):
    nc = tc.nc
    with ExitStack() as ctx:
        const = ctx.enter_context(tc.tile_pool(name="const", bufs=1))
        apool = ctx.enter_context(tc.tile_pool(name="apool", bufs=5))
        mpool = ctx.enter_context(tc.tile_pool(name="mpool", bufs=7))
        opool = ctx.enter_context(tc.tile_pool(name="opool", bufs=5))
        upool = ctx.enter_context(tc.tile_pool(name="upool", bufs=5))
        ppool = ctx.enter_context(tc.tile_pool(name="ppool", bufs=3))
        gpool = ctx.enter_context(tc.tile_pool(name="gpool", bufs=4))
        cpool = ctx.enter_context(tc.tile_pool(name="cpool", bufs=5))
        psT = ctx.enter_context(tc.psum_pool(name="psT", bufs=3))
        psP = ctx.enter_context(tc.psum_pool(name="psP", bufs=2))
        psM = ctx.enter_context(tc.psum_pool(name="psM", bufs=3))
        ctx.enter_context(tc.manual_schedule())

        xas = {}
        xms = {}

        def load_attn(b, fine):
            xa = apool.tile([P, L, J, KL], BF16, name="xa")
            xas[b] = xa
            src = attn_cache[:, b, 1:POS, :, :].rearrange("l (p j) h d -> p l (j h d)", j=J)
            dst = xa[:].rearrange("p l j k -> p l (j k)")
            if fine:
                return [(dst[:, l, :], src[:, l, :]) for l in range(L)]
            return [(dst, src)]

        def load_mlp(b, fine):
            xm = mpool.tile([P, M, J, DM], BF16, name="xm")
            xms[b] = xm
            src = mlp_cache[:, b, 1:POS, :].rearrange("m (p j) n -> p m (j n)", j=J)
            dst = xm[:].rearrange("p m j n -> p m (j n)")
            if fine:
                return [(dst[:, m, :], src[:, m, :]) for m in range(M)]
            return [(dst, src)]

        def issue(pairs):
            for dst, src in pairs:
                nc.sync.dma_start(out=dst, in_=src)

        mrow = const.tile([P, NAM + B * M], BF16)
        nc.vector.memset(mrow[:], 0.0)
        arow = const.tile([P, DM], BF16)
        nc.gpsimd.memset(arow[:], 0.0)
        rows = const.tile([P, DM], BF16)
        nc.gpsimd.memset(rows[:], 0.0)
        first_row = const.tile([P, P], BF16)
        nc.vector.memset(first_row[:], 0.0)
        nc.vector.memset(first_row[0:1, :], 1.0)
        nc.sync.dma_start(out=mrow[0:1, 0:NAM], in_=attn_mask.rearrange("b l h -> (b l h)").unsqueeze(0))
        nc.sync.dma_start(out=arow[0:L, :], in_=modal_attention.rearrange("l h d -> l (h d)"))
        wraw = mpool.tile([P, L, 4, DM], BF16, name="xm")
        wsrc = W_O.rearrange("l h d n -> (l h d) n").rearrange("(l p t) n -> p l (t n)", l=L, p=P, t=4)
        wdst = wraw[:].rearrange("p l t n -> p l (t n)")
        a0 = load_attn(0, True)
        m0 = load_mlp(0, True)
        nc.scalar.dma_start(out=a0[0][0], in_=a0[0][1])
        nc.scalar.dma_start(out=mrow[0:1, NAM:], in_=mlp_mask.rearrange("b m -> (b m)").unsqueeze(0))
        nc.scalar.dma_start(out=rows[R_MLP : R_MLP + M, :], in_=modal_mlp)
        nc.scalar.dma_start(out=rows[R_PB : R_PB + L, :], in_=post_bias)
        issue([(wdst[:, 0, :], wsrc[:, 0, :]), a0[1], (wdst[:, 1, :], wsrc[:, 1, :])])
        a1 = load_attn(1, True)
        issue(a1)
        issue([m0[1], m0[0], m0[2]])
        o8 = const.tile([B, DM], BF16)
        nc.sync.dma_start(out=o8[:], in_=orig_in[:, 0, :])
        for b in range(2, AHEAD):
            issue(load_attn(b, False))
            issue(load_mlp(b - 1, False))

        identb = const.tile([P, P], BF16)
        make_identity(nc, identb[:])
        ident = const.tile([P, P], F32)
        make_identity(nc, ident[:])
        off = const.tile([P, H], F32)
        nc.gpsimd.iota(off[:], pattern=[[-16, H]], base=0, channel_multiplier=1, allow_small_or_imprecise_dtypes=True)
        warm = const.tile([P, 1], F32)
        nc.scalar.activation(out=warm[:], in_=identb[:, 0:1], func=ACT.Identity, scale=1.0)

        spread = psM.tile([P, NAM], F32, name="pm")
        nc.tensor.matmul(out=spread[:], lhsT=first_row[:], rhs=mrow[:, 0:NAM], start=True, stop=True)
        att = psP.tile([P, 4, P], BF16, name="pp")
        for t in range(4):
            nc.tensor.transpose(out=att[:, t, :], in_=arow[:, t : 4 * P : 4], identity=identb[:])
        low = const.tile([P, H], F32)
        nc.vector.tensor_scalar(out=low[:], in0=off[:], scalar1=15.0, scalar2=None, op0=ALU.is_le)
        head = const.tile([P, H], F32)
        nc.vector.scalar_tensor_tensor(out=head[:], in0=off[:], scalar=0.0, in1=low[:], op0=ALU.is_ge, op1=ALU.mult)
        sel = const.tile([P, B * L, H], F32)
        nc.vector.tensor_tensor(
            out=sel[:],
            in0=spread[:].rearrange("p (c h) -> p c h", h=H),
            in1=head[:].unsqueeze(1).to_broadcast([P, B * L, H]),
            op=ALU.mult,
        )
        scl = const.tile([P, B, L], F32)
        nc.vector.reduce_sum(scl[:].rearrange("p b l -> p (b l)"), sel[:], axis=mybir.AxisListType.X)
        modalT = const.tile([P, L, 4], F32)
        nc.vector.tensor_copy(out=modalT[:], in_=att[:, :, 0:L].rearrange("p t l -> p l t"))
        om = const.tile([P, B * L], F32)
        nc.vector.tensor_scalar(
            out=om[:], in0=scl[:].rearrange("p b l -> p (b l)"), scalar1=-1.0, scalar2=1.0, op0=ALU.mult, op1=ALU.add
        )
        bia = const.tile([P, B, L, 4], F32)
        nc.vector.tensor_tensor(
            out=bia[:],
            in0=om[:].rearrange("p (b l) -> p b l", l=L).unsqueeze(3).to_broadcast([P, B, L, 4]),
            in1=modalT[:].unsqueeze(1).to_broadcast([P, B, L, 4]),
            op=ALU.mult,
        )
        mmf = const.tile([P, B, M], F32)
        diag = const.tile([P, B, P], BF16)
        cT = const.tile([P, NB, B], F32)

        def const_columns():
            spread_m = psM.tile([P, B * M], F32, name="pm")
            nc.tensor.matmul(out=spread_m[:], lhsT=first_row[:], rhs=mrow[:, NAM:], start=True, stop=True)
            nc.vector.tensor_copy(out=mmf[:].rearrange("p b m -> p (b m)"), in_=spread_m[:])
            nc.gpsimd.tensor_tensor(
                out=diag[:],
                in0=identb[:].unsqueeze(1).to_broadcast([P, B, P]),
                in1=mmf[:, :, 0:1].to_broadcast([P, B, P]),
                op=ALU.mult,
            )
            pc = psM.tile([P, NB, P], BF16, name="pm")
            for nb in range(NB):
                nc.tensor.transpose(out=pc[:, nb, :], in_=rows[:, P * nb : P * nb + P], identity=identb[:])
            rT = const.tile([P, NB, M + L], F32)
            nc.vector.tensor_copy(out=rT[:], in_=pc[:, :, R_MLP : R_MLP + M + L])
            omm = const.tile([P, B, M], F32)
            nc.vector.tensor_scalar(out=omm[:], in0=mmf[:], scalar1=-1.0, scalar2=1.0, op0=ALU.mult, op1=ALU.add)
            pbT = const.tile([P, NB], F32)
            nc.vector.reduce_sum(pbT[:], rT[:, :, M : M + L], axis=mybir.AxisListType.X)
            ct3 = const.tile([P, NB, B, M], F32)
            for nb in range(NB):
                nc.vector.tensor_tensor(
                    out=ct3[:, nb], in0=omm[:], in1=rT[:, nb : nb + 1, 0:M].to_broadcast([P, B, M]), op=ALU.mult
                )
            ct1 = const.tile([P, NB, B], F32)
            nc.vector.reduce_sum(ct1[:], ct3[:], axis=mybir.AxisListType.X)
            nc.vector.tensor_tensor(
                out=cT[:], in0=ct1[:], in1=pbT[:].unsqueeze(2).to_broadcast([P, NB, B]), op=ALU.add
            )

        wc = const.tile([P, L, DM], U32, align_bytes=64)
        ws = const.tile([P, L, DM], U8, align_bytes=64)

        wgs = {}

        def w_regroup(l):
            grp = gpool.tile([P, DM, 4], BF16, align_bytes=64, name="grp")
            wgs[l] = grp
            interleave(nc.vector.tensor_copy, grp[:], wraw[:, l])

        def w_quant(l):
            nc.vector.quantize_mx(
                out=wc[:, l, :].bitcast(FP8X4), scales=ws[:, l, :], in_=wgs[l][:].rearrange("p n t -> p (n t)")
            )

        banks = {}
        planes = {}
        grps = {}
        codes = {}
        pms = {}
        ups = {}
        pos = {}
        accs = {}

        def turn(h):
            b, l = divmod(h, L)
            for u in range(2):
                pt = psT.tile([P, J, P], F32, name="pt")
                banks[h, u] = pt
                for j in range(J):
                    nc.tensor.transpose(
                        out=pt[:, j, :], in_=xas[b][:, l, j, :].bitcast(F32)[:, u : 2 * P : 2], identity=ident[:]
                    )

        def blend(h):
            b, l = divmod(h, L)
            pl = ppool.tile([P, 4, J * P], BF16, name="pl")
            planes[h] = pl
            for u in range(2):
                ptv = banks[h, u][:].rearrange("p j r -> p (j r)").bitcast(BF16).rearrange("p (c e) -> p c e", e=2)
                for e in range(2):
                    nc.scalar.activation(
                        out=pl[:, 2 * u + e, :],
                        in_=ptv[:, :, e],
                        func=ACT.Identity,
                        bias=bia[:, b, l, 2 * u + e : 2 * u + e + 1],
                        scale=scl[:, b, l : l + 1],
                    )

        def regroup_scalar(h):
            grp = gpool.tile([P, J * P, 4], BF16, align_bytes=64, name="grp")
            grps[h] = grp
            if h >= FIRST_SPLIT:
                interleave(nc.scalar.copy, grp[:, V_COLUMNS:], planes[h][:, :, V_COLUMNS:])

        def regroup_vector(h):
            cols = V_COLUMNS if h >= FIRST_SPLIT else J * P
            interleave(nc.vector.tensor_copy, grps[h][:, 0:cols], planes[h][:, :, 0:cols])

        def quant(h):
            ac = cpool.tile([P, J * P], U32, align_bytes=64, name="ac")
            asc = cpool.tile([P, J * P], U8, align_bytes=64, name="asc")
            nc.vector.quantize_mx(out=ac[:].bitcast(FP8X4), scales=asc[:], in_=grps[h][:].rearrange("p c t -> p (c t)"))
            codes[h] = (ac, asc)

        def plain(b, j):
            on_pe = product_on_tensor(b, j)
            po = psP.tile([P, NB, P], F32, name="pp")
            pos[b, j] = po
            if on_pe:
                nc.tensor.matmul(
                    out=po[:].rearrange("p a n -> p (a n)"), lhsT=diag[:, b, :], rhs=xms[b][:, 0, j, :], start=True, stop=False
                )
            for nb in range(NB):
                nc.tensor.matmul(
                    out=po[:, nb, :],
                    lhsT=cT[:, nb, b : b + 1].to_broadcast([P, P]),
                    rhs=ident[:],
                    start=not on_pe,
                    stop=(not on_pe or nb == NB - 1),
                    is_transpose=True,
                )

        def mx(b, j):
            pm = psM.tile([P, DM], F32, name="pm")
            pms[b, j] = pm
            for l in range(L):
                ac, asc = codes[L * b + l]
                nc.tensor.matmul_mx(
                    out=pm[:],
                    lhsT=ac[:, P * j : P * j + P].bitcast(FP8X4),
                    lhsT_scale=asc[:, P * j : P * j + P],
                    rhs=wc[:, l, :].bitcast(FP8X4),
                    rhs_scale=ws[:, l, :],
                    start=(l == 0),
                    stop=(l == L - 1),
                )

        def term(out_, b, m, j, other):
            nc.vector.scalar_tensor_tensor(
                out=out_, in0=xms[b][:, m, j, :], scalar=mmf[:, b, m : m + 1], in1=other, op0=ALU.mult, op1=ALU.add
            )

        def upper(b, j):
            half, jj = divmod(j, 2)
            if jj == 0:
                up = upool.tile([P, 2, DM], F32, name="up")
                ups[b, half] = up
            term(ups[b, half][:, jj, :], b, 2, j, pos[b, j][:].rearrange("p a n -> p (a n)"))

        def middle(b, j):
            up = ups[b, j // 2][:, j % 2, :]
            if not product_on_tensor(b, j):
                term(up, b, 0, j, up)
            if summed_on_vector(b):
                term(up, b, 1, j, up)

        def lower(b, j):
            half, jj = divmod(j, 2)
            if summed_on_vector(b):
                up = ups[b, half][:, jj, :]
                nc.vector.tensor_tensor(out=up, in0=up, in1=pms[b, j][:], op=ALU.add)
                dst = out[b, 1:POS, :].rearrange("(p j) n -> p j n", j=J)
                nc.sync.dma_start(out=dst[:, j, :], in_=up)
                return
            if jj == 0:
                acc = opool.tile([P, 2, DM], F32, name="acc")
                accs[b, half] = acc
            term(accs[b, half][:, jj, :], b, 1, j, pms[b, j][:])

        def finish(b, half):
            if summed_on_vector(b):
                return
            acc = accs[b, half]
            for jj in range(2):
                for c in range(0, DM, PIECE):
                    piece = acc[:, jj, c : c + PIECE]
                    nc.gpsimd.tensor_tensor(out=piece, in0=piece, in1=ups[b, half][:, jj, c : c + PIECE], op=ALU.add)
            dst = out[b, 1:POS, :].rearrange("(p j) n -> p j n", j=J)
            nc.sync.dma_start(out=dst[:, 2 * half : 2 * half + 2, :], in_=acc[:])

        turn(0)
        blend(0)
        regroup_scalar(0)
        w_regroup(0)
        const_columns()
        w_quant(0)
        o8f = const.tile([B, DM], F32)
        nc.gpsimd.tensor_copy(out=o8f[:], in_=o8[:])

        for h in range(L * B + 3):
            bx, half = divmod(h - 2, 2)
            js = (2 * half, 2 * half + 1) if 0 <= bx < B else ()
            if h + 1 < L * B:
                turn(h + 1)
                blend(h + 1)
                regroup_scalar(h + 1)
            for j in js:
                mx(bx, j)
            if 1 <= h <= L * B:
                b, first = divmod(2 * (h - 1), J)
                for j in (first, first + 1):
                    plain(b, j)
            if h < L * B:
                regroup_vector(h)
            if h == 0:
                w_regroup(1)
            for j in js:
                upper(bx, j)
            if h < L * B:
                quant(h)
            if h == 0:
                w_quant(1)
            for j in js:
                middle(bx, j)
            for j in js:
                lower(bx, j)
            if 0 <= h - 3 < L * B:
                finish(*divmod(h - 3, 2))
            if h % 2 == 1:
                b = h // 2
                if b + AHEAD < B:
                    issue(load_attn(b + AHEAD, False))
                if b + AHEAD - 1 < B:
                    issue(load_mlp(b + AHEAD - 1, False))
            if h == 4:
                nc.sync.dma_start(out=out[:, 0, :], in_=o8f[:])
